import numpy as np
import ml_dtypes


def mxq(x, axis, fmt="e4m3"):
    dtype, down = {"e4m3": (ml_dtypes.float8_e4m3fn, 7), "e5m2": (ml_dtypes.float8_e5m2, 14)}[fmt]
    v = np.moveaxis(np.asarray(x, np.float32).astype(ml_dtypes.bfloat16).astype(np.float64), axis, -1)
    blocks = v.reshape(v.shape[:-1] + (-1, 32))
    amax = np.abs(blocks).max(-1, keepdims=True)
    byte = np.maximum(np.where(amax > 0, np.frexp(amax)[1] - 1 + 127, 0) - down, 1)
    scale = np.exp2(byte - 127.0)
    codes = (blocks / scale).astype(np.float32).astype(dtype).astype(np.float64)
    return np.moveaxis((codes * scale).reshape(v.shape), -1, axis)


WIDE = False


def mx_kscale(k):
    if not WIDE:
        return np.ones(k)
    levels = np.array([10, -10, 5, -5, 0])
    a = np.random.permutation(np.resize(levels, k // 512 * 4)).reshape(k // 512, 4)
    idx = np.arange(k)
    return np.exp2(a[idx // 512, idx % 128 // 32])


BF16 = ml_dtypes.bfloat16


def bf(x):
    return np.asarray(x, np.float32).astype(BF16)


def f64(x):
    return np.asarray(x).astype(np.float64)


B, CI, H, W, C, KS = 1, 256, 64, 64, 512, 3
GROUPS = KS * KS
PAD = KS // 2
ICPG = CI // GROUPS
OCPG = C // GROUPS


def shift_conv(x, out_full):
    b, c, h, w = x.shape
    in_ch = c - c % GROUPS
    in_cpg = in_ch // GROUPS
    out_ch = out_full - out_full % GROUPS
    out_cpg = out_ch // GROUPS
    miss = out_full - out_ch
    s = x[:, :in_ch].reshape(b, GROUPS, in_cpg, h, w).sum(axis=2)
    sp = np.pad(s, ((0, 0), (0, 0), (PAD, PAD), (PAD, PAD)))
    offsets = [(i, j) for i in range(KS) for j in range(KS)]
    shifts = np.stack([sp[:, g, i:i + h, j:j + w] for g, (i, j) in enumerate(offsets)], axis=1)
    out = np.repeat(shifts, out_cpg, axis=1)
    if miss > 0:
        centre = out[:, out_ch // 2:out_ch // 2 + 1]
        out = np.concatenate([out, np.broadcast_to(centre, (b, miss, h, w))], axis=1)
    return out


def setup_inputs():
    u = np.sort(mx_kscale(C))[np.round(np.linspace(0, C - 1, GROUPS)).astype(int)]
    ux = np.concatenate([np.repeat(u, ICPG), np.ones(CI - GROUPS * ICPG)])
    uc = np.concatenate([np.repeat(u, OCPG), np.repeat(u[(GROUPS * OCPG // 2) // OCPG], C - GROUPS * OCPG)])
    return {"x": bf(np.random.standard_normal((B, CI, H, W)) / np.sqrt(ICPG) * ux[None, :, None, None]),
            "w_pw": bf(np.random.standard_normal((C, C)) / np.sqrt(C) / uc[None, :])}


def reference(x, w_pw):
    out_full = w_pw.shape[0]
    shifted = shift_conv(f64(x), out_full)
    b, c, h, w = shifted.shape
    sq = mxq(shifted, 1, "e4m3").reshape(b, c, h * w)
    return (mxq(f64(w_pw), 1, "e4m3") @ sq).reshape(b, out_full, h, w)

@@ -1,0 +1,259 @@
+from contextlib import ExitStack
+
+import concourse.mybir as mybir
+from concourse.masks import make_identity
+
+FLOPS = 2 * 512 * 512 * 4096
+
+BF16 = mybir.dt.bfloat16
+F32 = mybir.dt.float32
+I32 = mybir.dt.int32
+U8 = mybir.dt.uint8
+U32 = mybir.dt.uint32
+FP8X4 = mybir.dt.float8_e4m3fn_x4
+ADD = mybir.AluOpType.add
+SUB = mybir.AluOpType.subtract
+MULT = mybir.AluOpType.mult
+AX = mybir.AxisListType.X
+
+P = 128
+NG = 9
+ROW = 1024
+HALF = 512
+NCHUNK = 8
+
+
+def x_base(g):
+    shift = 64 * (g // 3 - 1) + (g % 3 - 1)
+    if g == 0:
+        return ROW + shift
+    return (28 * 4 * g - 16) * ROW + shift
+
+
+def tile_shiftconv_kernel(tc, x, w_pw, out):
+    nc = tc.nc
+    with ExitStack() as ctx:
+        keep = ctx.enter_context(tc.tile_pool(name="keep", bufs=1))
+        ps_sum = ctx.enter_context(tc.psum_pool(name="ps_sum", bufs=1))
+        ps_aux = ctx.enter_context(tc.psum_pool(name="ps_aux", bufs=2))
+        ps_mx = ctx.enter_context(tc.psum_pool(name="ps_mx", bufs=5))
+        ctx.enter_context(tc.manual_schedule())
+
+        x_flat = x.rearrange("b c h w -> (b c h w)")
+        out_v = out.rearrange("b (o t) h w -> o (b t) (h w)", t=4)
+
+        xfix = keep.tile([P, ROW], BF16, name="xfix")
+        nc.vector.memset(xfix[:].bitcast(I32), 0)
+        nc.scalar.dma_start(
+            out=xfix[0:1, 65:ROW], in_=x_flat[0 : ROW - 65].rearrange("(o n) -> o n", o=1)
+        )
+        xt = {}
+
+        def load_piece(pi):
+            for g in range(NG):
+                t = keep.tile([P, HALF], BF16, name="x%d_%d" % (g, pi))
+                b = x_base(g)
+                src = x_flat[b : b + P * ROW].rearrange("(r l) -> r l", l=ROW)
+                nc.sync.dma_start(out=t[:], in_=src[:, HALF * pi : HALF * (pi + 1)])
+                xt[(g, pi)] = t
+
+        load_piece(0)
+        w_sb = keep.tile([P, 4, 512], BF16, name="w_sb")
+        nc.sync.dma_start(out=w_sb[:], in_=w_pw.rearrange("(o t) c -> o t c", t=4))
+        load_piece(1)
+
+        ident_f = keep.tile([P, P], F32, name="ident_f")
+        make_identity(nc, ident_f[:])
+        s1 = []
+        for pi in range(2):
+            t = keep.tile([P, 4, P], BF16, name="s1_%d" % pi)
+            nc.gpsimd.memset(t[:], 0.0)
+            s1.append(t)
+        warm = keep.tile([P, 2], F32, name="warm")
+        nc.vector.memset(warm[:, 0:1], 0.0)
+        nc.scalar.copy(out=warm[:, 1:2], in_=warm[:, 0:1])
+
+        ident_b = keep.tile([P, P], BF16, name="ident_b")
+        nc.vector.tensor_copy(out=ident_b[:], in_=ident_f[:])
+        selr = keep.tile([P, 2, 4], F32, name="selr")
+        nc.vector.tensor_reduce(
+            out=selr[:, 0, :], in_=ident_f[:, 0:112].rearrange("k (c e) -> k e c", e=4), axis=AX, op=ADD
+        )
+        nc.vector.tensor_reduce(
+            out=selr[:, 1, :], in_=ident_f[:, 16:128].rearrange("k (c e) -> k e c", e=4), axis=AX, op=ADD
+        )
+        sel0 = keep.tile([P, 4], BF16, name="sel0")
+        nc.vector.tensor_copy(out=sel0[:, 1:4], in_=selr[:, 0, 0:3])
+        nc.vector.tensor_tensor(out=sel0[:, 0:1], in0=selr[:, 0, 3:4], in1=ident_f[:, 111:112], op=SUB)
+        selg = keep.tile([P, 4], BF16, name="selg")
+        nc.vector.tensor_copy(out=selg[:], in_=selr[:, 1, :])
+
+        ab = keep.tile([P, 2], F32, name="ab")
+        nc.vector.tensor_tensor(out=ab[:, 0:1], in0=ident_f[:, 0:1], in1=ident_f[:, 64:65], op=ADD)
+        nc.vector.tensor_tensor(out=ab[:, 1:2], in0=ident_f[:, 63:64], in1=ident_f[:, 127:128], op=ADD)
+        nab = keep.tile([P, 2], F32, name="nab")
+        nc.vector.tensor_scalar(out=nab[:], in0=ab[:], scalar1=-1.0, scalar2=1.0, op0=MULT, op1=ADD)
+        mask = keep.tile([P, 2, 4, 36], F32, name="mask")
+        nc.vector.memset(mask[:], 1.0)
+        mv = mask[:].rearrange("p a q (c i j) -> p (a q c i) j", i=3, j=3)
+        nc.vector.tensor_copy(out=mv[:, :, 0], in_=nab[:, 0:1].to_broadcast([P, 96]))
+        nc.vector.tensor_copy(out=mv[:, :, 2], in_=nab[:, 1:2].to_broadcast([P, 96]))
+        nc.vector.memset(mask[0:64, 0, 0, 0:3], 0.0)
+        nc.vector.memset(mask[64:128, 1, 3, 33:36], 0.0)
+
+        spread = keep.tile([P, 4, P], BF16, name="spread")
+        idg = ident_f[:, 0:36].rearrange("k (t g) -> k t g", g=NG)
+        nc.vector.tensor_copy(
+            out=spread[:, :, 0:126].rearrange("k t (g r) -> k t g r", r=14),
+            in_=idg.unsqueeze(3).to_broadcast([P, 4, NG, 14]),
+        )
+        nc.vector.tensor_copy(out=spread[:, :, 126:128], in_=idg[:, :, 4:5].to_broadcast([P, 4, 2]))
+
+        sums = ps_sum.tile([P, 2, 4, NG, 4], F32, name="sums")
+        stt = {}
+        pts = {}
+        tps = {}
+        tbs = {}
+        groupeds = {}
+        codes = {}
+        scales = {}
+        accs = {}
+        ress = {}
+
+        def group_sums(pi, groups):
+            for g in groups:
+                for ct in range(4):
+                    dst = sums[:, pi, ct, g, :]
+                    lhs = xt[(g, pi)][:, P * ct : P * (ct + 1)]
+                    if g == 0:
+                        nc.tensor.matmul(dst, lhsT=lhs, rhs=sel0[:], start=True, stop=False)
+                        nc.tensor.matmul(
+                            dst,
+                            lhsT=xfix[:, HALF * pi + P * ct : HALF * pi + P * (ct + 1)],
+                            rhs=ident_b[:, 0:4],
+                            start=False,
+                            stop=True,
+                        )
+                    else:
+                        nc.tensor.matmul(dst, lhsT=lhs, rhs=selg[:], start=True, stop=True)
+
+        def round_sums(pi):
+            nc.vector.tensor_tensor(
+                out=s1[pi][:, :, 0:36],
+                in0=sums[:, pi].rearrange("p c g q -> p q (c g)"),
+                in1=mask[:, pi],
+                op=MULT,
+            )
+
+        def flip_sums(pi):
+            pt = ps_aux.tile([P, 4, P], BF16, tag="aux", name="pt%d" % pi)
+            for q in range(4):
+                nc.tensor.transpose(pt[:, q, :], s1[pi][:, q, :], ident_b[:])
+            pts[pi] = pt
+
+        def keep_flipped(pi):
+            t = keep.tile([P, 4, P], BF16, name="stt%d" % pi)
+            nc.scalar.copy(out=t[:], in_=pts[pi][:])
+            stt[pi] = t
+
+        def spread_chunk(c):
+            tp = ps_aux.tile([P, 4, P], BF16, tag="aux", name="tp%d" % c)
+            for tl in range(4):
+                nc.tensor.matmul(
+                    tp[:, tl, :], lhsT=spread[:, tl, :], rhs=stt[c // 4][:, c % 4, :], start=True, stop=True
+                )
+            tps[c] = tp
+
+        def copy_tb(c):
+            tb = keep.tile([P, 512], BF16, name="tb%d" % c)
+            nc.scalar.copy(out=tb[:], in_=tps[c][:].rearrange("p t n -> p (t n)"))
+            tbs[c] = tb
+
+        def expand(c):
+            grouped = keep.tile([P, 512, 4], BF16, name="grouped%d" % c, align_bytes=64)
+            nc.vector.tensor_copy(out=grouped[:], in_=tbs[c][:].unsqueeze(2).to_broadcast([P, 512, 4]))
+            groupeds[c] = grouped
+
+        def quantise(c):
+            cd = keep.tile([P, 512], U32, name="codes%d" % c, align_bytes=64)
+            sc = keep.tile([P, 512], U8, name="scales%d" % c, align_bytes=64)
+            nc.vector.quantize_mx(
+                out=cd[:].bitcast(FP8X4),
+                scales=sc[:],
+                in_=groupeds[c][:].rearrange("p n j -> p (n j)"),
+            )
+            codes[c] = cd
+            scales[c] = sc
+
+        def multiply(c):
+            for ot in range(4):
+                acc = ps_mx.tile([P, 512], F32, tag="acc", name="acc%d_%d" % (c, ot))
+                nc.tensor.matmul_mx(
+                    out=acc[:],
+                    lhsT=w_codes[:, P * ot : P * (ot + 1)].bitcast(FP8X4),
+                    lhsT_scale=w_scales[:, P * ot : P * (ot + 1)],
+                    rhs=codes[c][:].bitcast(FP8X4),
+                    rhs_scale=scales[c][:],
+                    start=True,
+                    stop=True,
+                )
+                accs[(c, ot)] = acc
+
+        def evict(c, ot, on_vector):
+            res = keep.tile([P, 512], F32, name="res%d_%d" % (c, ot))
+            if on_vector:
+                nc.vector.tensor_copy(out=res[:], in_=accs[(c, ot)][:])
+            else:
+                nc.scalar.copy(out=res[:], in_=accs[(c, ot)][:])
+            n0 = ROW * (c % 4) + HALF * (c // 4)
+            nc.sync.dma_start(out=out_v[:, ot, n0 : n0 + 512], in_=res[:])
+
+        group_sums(0, range(NG))
+        round_sums(0)
+        flip_sums(0)
+        keep_flipped(0)
+        spread_chunk(0)
+        copy_tb(0)
+
+        gw = keep.tile([P, 4, P, 2], F32, name="gw", align_bytes=64)
+        for b in range(2):
+            wt = ps_mx.tile([P, 2, 2, P], F32, tag="acc", name="wt%d" % b)
+            for tl in range(2):
+                words = w_sb[:, 2 * b + tl, :].bitcast(F32).rearrange("o (p u) -> o u p", u=2)
+                for u in range(2):
+                    nc.tensor.transpose(wt[:, tl, u, :], words[:, u, :], ident_f[:])
+            nc.scalar.copy(out=gw[:, 2 * b : 2 * b + 2, :, :], in_=wt[:].rearrange("p t u o -> p t o u"))
+        w_codes = keep.tile([P, 512], U32, name="w_codes", align_bytes=64)
+        w_scales = keep.tile([P, 512], U8, name="w_scales", align_bytes=64)
+
+        expand(0)
+        nc.vector.quantize_mx(
+            out=w_codes[:].bitcast(FP8X4),
+            scales=w_scales[:],
+            in_=gw[:].rearrange("p t o u -> p (t o u)").bitcast(BF16),
+        )
+        quantise(0)
+        spread_chunk(1)
+        copy_tb(1)
+        group_sums(1, range(0, 6))
+
+        for c in range(NCHUNK):
+            last = c == NCHUNK - 1
+            multiply(c)
+            evict(c, 0, False)
+            if not last:
+                expand(c + 1)
+            evict(c, 1, True)
+            evict(c, 2, False)
+            evict(c, 3, last)
+            if c + 2 < NCHUNK:
+                spread_chunk(c + 2)
+                copy_tb(c + 2)
+            if c == 0:
+                group_sums(1, range(6, NG))
+            if c == 1:
+                round_sums(1)
+                flip_sums(1)
+                keep_flipped(1)
+            if not last:
+                quantise(c + 1)

@@ -12,22 +12,25 @@ U8 = mybir.dt.uint8
 U32 = mybir.dt.uint32
 FP8X4 = mybir.dt.float8_e4m3fn_x4
 ADD = mybir.AluOpType.add
-SUB = mybir.AluOpType.subtract
 MULT = mybir.AluOpType.mult
 AX = mybir.AxisListType.X
 
 P = 128
 NG = 9
-ROW = 1024
-HALF = 512
+CH = 4096
+QUARTER = 1024
+CHUNK = 512
 NCHUNK = 8
 
 
-def x_base(g):
-    shift = 64 * (g // 3 - 1) + (g % 3 - 1)
+def shift_of(g):
+    return 64 * (g // 3 - 1) + (g % 3 - 1)
+
+
+def first_channel(g):
     if g == 0:
-        return ROW + shift
-    return (28 * 4 * g - 16) * ROW + shift
+        return 0
+    return 28 * g - 4
 
 
 def tile_shiftconv_kernel(tc, x, w_pw, out):
@@ -42,39 +45,50 @@ def tile_shiftconv_kernel(tc, x, w_pw, out):
         x_flat = x.rearrange("b c h w -> (b c h w)")
         out_v = out.rearrange("b (o t) h w -> o (b t) (h w)", t=4)
 
-        xfix = keep.tile([P, ROW], BF16, name="xfix")
-        nc.vector.memset(xfix[:].bitcast(I32), 0)
-        nc.scalar.dma_start(
-            out=xfix[0:1, 65:ROW], in_=x_flat[0 : ROW - 65].rearrange("(o n) -> o n", o=1)
-        )
-        xt = {}
-
-        def load_piece(pi):
-            for g in range(NG):
-                t = keep.tile([P, HALF], BF16, name="x%d_%d" % (g, pi))
-                b = x_base(g)
-                src = x_flat[b : b + P * ROW].rearrange("(r l) -> r l", l=ROW)
-                nc.sync.dma_start(out=t[:], in_=src[:, HALF * pi : HALF * (pi + 1)])
-                xt[(g, pi)] = t
-
-        load_piece(0)
+        xk = {}
+        for q in range(4):
+            for k in range(2):
+                xk[(k, q)] = keep.tile([P, QUARTER], BF16, name="xk%d_%d" % (k, q))
+        x8 = keep.tile([P, QUARTER], BF16, name="x8")
         w_sb = keep.tile([P, 4, 512], BF16, name="w_sb")
+        nc.vector.memset(xk[(0, 0)][:, 0:80].bitcast(I32), 0)
+
+        def load_group(g, q):
+            dst = xk[(g // 4, q)]
+            b = first_channel(g) * CH + QUARTER * q + shift_of(g)
+            if b < 0:
+                src = x_flat[0 : 32 * CH].rearrange("(c r) -> c r", r=CH)
+                nc.sync.dma_start(out=dst[g % 4 : P : 4, -b:QUARTER], in_=src[:, 0 : QUARTER + b])
+            else:
+                src = x_flat[b : b + 32 * CH].rearrange("(c r) -> c r", r=CH)
+                nc.sync.dma_start(out=dst[g % 4 : P : 4, :], in_=src[:, 0:QUARTER])
+
+        for g in (4, 5, 6, 7, 0, 1, 2, 3):
+            load_group(g, 0)
+        b8 = first_channel(8) * CH + shift_of(8)
+        nc.sync.dma_start(out=x8[:], in_=x_flat[b8 : b8 + P * QUARTER].rearrange("(r l) -> r l", l=QUARTER))
         nc.sync.dma_start(out=w_sb[:], in_=w_pw.rearrange("(o t) c -> o t c", t=4))
-        load_piece(1)
+        for q in range(1, 4):
+            for g in range(8):
+                load_group(g, q)
 
         ident_f = keep.tile([P, P], F32, name="ident_f")
         make_identity(nc, ident_f[:])
-        s1 = []
-        for pi in range(2):
-            t = keep.tile([P, 4, P], BF16, name="s1_%d" % pi)
-            nc.gpsimd.memset(t[:], 0.0)
-            s1.append(t)
+        direct_w = keep.tile([P, 3, P], BF16, name="direct_w")
+        nc.gpsimd.memset(direct_w[:], 0.0)
+        m2 = keep.tile([P, 2, CHUNK], F32, name="m2")
+        nc.gpsimd.memset(m2[:], 1.0)
+        mask = keep.tile([P, 3, 2, 36], F32, name="mask")
+        nc.gpsimd.memset(mask[:], 1.0)
+        s1 = {}
+        for q in range(1, 4):
+            s1[q] = keep.tile([P, 2, P], BF16, name="s1_%d" % q)
+            nc.gpsimd.memset(s1[q][:], 0.0)
+
         warm = keep.tile([P, 2], F32, name="warm")
         nc.vector.memset(warm[:, 0:1], 0.0)
         nc.scalar.copy(out=warm[:, 1:2], in_=warm[:, 0:1])
 
-        ident_b = keep.tile([P, P], BF16, name="ident_b")
-        nc.vector.tensor_copy(out=ident_b[:], in_=ident_f[:])
         selr = keep.tile([P, 2, 4], F32, name="selr")
         nc.vector.tensor_reduce(
             out=selr[:, 0, :], in_=ident_f[:, 0:112].rearrange("k (c e) -> k e c", e=4), axis=AX, op=ADD
@@ -82,25 +96,45 @@ def tile_shiftconv_kernel(tc, x, w_pw, out):
         nc.vector.tensor_reduce(
             out=selr[:, 1, :], in_=ident_f[:, 16:128].rearrange("k (c e) -> k e c", e=4), axis=AX, op=ADD
         )
-        sel0 = keep.tile([P, 4], BF16, name="sel0")
-        nc.vector.tensor_copy(out=sel0[:, 1:4], in_=selr[:, 0, 0:3])
-        nc.vector.tensor_tensor(out=sel0[:, 0:1], in0=selr[:, 0, 3:4], in1=ident_f[:, 111:112], op=SUB)
-        selg = keep.tile([P, 4], BF16, name="selg")
-        nc.vector.tensor_copy(out=selg[:], in_=selr[:, 1, :])
+        nc.vector.tensor_copy(out=direct_w[:, 1, 56:112].rearrange("k (e r) -> k e r", r=14),
+                              in_=selr[:, 1, :].unsqueeze(2).to_broadcast([P, 4, 14]))
+        nc.vector.tensor_copy(out=direct_w[:, 1, 126:128], in_=selr[:, 1, 0:1].to_broadcast([P, 2]))
+        nc.vector.tensor_copy(out=direct_w[:, 0, 0:14], in_=selr[:, 0, 0:1].to_broadcast([P, 14]))
+        nc.vector.tensor_copy(out=direct_w[:, 0, 14:56].rearrange("k (e r) -> k e r", r=14),
+                              in_=selr[:, 1, 1:4].unsqueeze(2).to_broadcast([P, 3, 14]))
+        nc.vector.tensor_copy(out=direct_w[:, 2, 112:126], in_=selr[:, 1, 0:1].to_broadcast([P, 14]))
 
+        gm = keep.tile([P, NG], F32, name="gm")
+        nc.vector.tensor_reduce(out=gm[:], in_=ident_f[:, 0:126].rearrange("p (g r) -> p g r", r=14), axis=AX, op=ADD)
+        nc.vector.tensor_tensor(out=gm[:, 4:5], in0=gm[:, 4:5], in1=ident_f[:, 126:127], op=ADD)
+        nc.vector.tensor_tensor(out=gm[:, 4:5], in0=gm[:, 4:5], in1=ident_f[:, 127:128], op=ADD)
+        csrs = keep.tile([P, 2, 3], F32, name="csrs")
+        nc.vector.tensor_reduce(out=csrs[:, 0, :], in_=gm[:].rearrange("p (i j) -> p j i", j=3), axis=AX, op=ADD)
+        nc.vector.tensor_reduce(out=csrs[:, 1, :], in_=gm[:].rearrange("p (i j) -> p i j", j=3), axis=AX, op=ADD)
+        zz = keep.tile([P, 2, 3], F32, name="zz")
+        nc.vector.tensor_scalar(out=zz[:], in0=csrs[:], scalar1=-1.0, scalar2=1.0, op0=MULT, op1=ADD)
+        m2v = m2[:].rearrange("p a (h w) -> p (a h) w", w=64)
+        nc.vector.tensor_copy(out=m2v[:, :, 0], in_=zz[:, 0, 0:1].to_broadcast([P, 16]))
+        nc.vector.tensor_copy(out=m2v[:, :, 63], in_=zz[:, 0, 2:3].to_broadcast([P, 16]))
+        nc.vector.tensor_scalar(out=m2[:, 0, 0:64], in0=m2[:, 0, 0:64], scalar1=zz[:, 1, 0:1], scalar2=None, op0=MULT)
+
+        sel_k = []
+        for k in range(2):
+            sel_k.append(keep.tile([P, 4], BF16, name="sel_k%d" % k))
+        nc.vector.tensor_copy(out=sel_k[1][:], in_=selr[:, 1, :])
+        nc.vector.tensor_copy(out=sel_k[0][:, 0:1], in_=selr[:, 0, 0:1])
+        nc.vector.tensor_copy(out=sel_k[0][:, 1:4], in_=selr[:, 1, 1:4])
+        ident_b = keep.tile([P, P], BF16, name="ident_b")
+        nc.vector.tensor_copy(out=ident_b[:], in_=ident_f[:])
         ab = keep.tile([P, 2], F32, name="ab")
         nc.vector.tensor_tensor(out=ab[:, 0:1], in0=ident_f[:, 0:1], in1=ident_f[:, 64:65], op=ADD)
         nc.vector.tensor_tensor(out=ab[:, 1:2], in0=ident_f[:, 63:64], in1=ident_f[:, 127:128], op=ADD)
         nab = keep.tile([P, 2], F32, name="nab")
         nc.vector.tensor_scalar(out=nab[:], in0=ab[:], scalar1=-1.0, scalar2=1.0, op0=MULT, op1=ADD)
-        mask = keep.tile([P, 2, 4, 36], F32, name="mask")
-        nc.vector.memset(mask[:], 1.0)
-        mv = mask[:].rearrange("p a q (c i j) -> p (a q c i) j", i=3, j=3)
-        nc.vector.tensor_copy(out=mv[:, :, 0], in_=nab[:, 0:1].to_broadcast([P, 96]))
-        nc.vector.tensor_copy(out=mv[:, :, 2], in_=nab[:, 1:2].to_broadcast([P, 96]))
-        nc.vector.memset(mask[0:64, 0, 0, 0:3], 0.0)
-        nc.vector.memset(mask[64:128, 1, 3, 33:36], 0.0)
-
+        mv = mask[:].rearrange("p a h (c i j) -> p (a h c i) j", i=3, j=3)
+        nc.vector.tensor_copy(out=mv[:, :, 0], in_=nab[:, 0:1].to_broadcast([P, 72]))
+        nc.vector.tensor_copy(out=mv[:, :, 2], in_=nab[:, 1:2].to_broadcast([P, 72]))
+        nc.vector.memset(mask[64:128, 2, 1, 33:36], 0.0)
         spread = keep.tile([P, 4, P], BF16, name="spread")
         idg = ident_f[:, 0:36].rearrange("k (t g) -> k t g", g=NG)
         nc.vector.tensor_copy(
@@ -109,7 +143,11 @@ def tile_shiftconv_kernel(tc, x, w_pw, out):
         )
         nc.vector.tensor_copy(out=spread[:, :, 126:128], in_=idg[:, :, 4:5].to_broadcast([P, 4, 2]))
 
-        sums = ps_sum.tile([P, 2, 4, NG, 4], F32, name="sums")
+        sums = ps_sum.tile([P, 3, 2, 36], F32, name="sums")
+        gw = keep.tile([P, 4, P, 2], F32, name="gw", align_bytes=64)
+        w_codes = keep.tile([P, 512], U32, name="w_codes", align_bytes=64)
+        w_scales = keep.tile([P, 512], U8, name="w_scales", align_bytes=64)
+        wts = {}
         stt = {}
         pts = {}
         tps = {}
@@ -118,65 +156,94 @@ def tile_shiftconv_kernel(tc, x, w_pw, out):
         codes = {}
         scales = {}
         accs = {}
-        ress = {}
 
-        def group_sums(pi, groups):
-            for g in groups:
-                for ct in range(4):
-                    dst = sums[:, pi, ct, g, :]
-                    lhs = xt[(g, pi)][:, P * ct : P * (ct + 1)]
-                    if g == 0:
-                        nc.tensor.matmul(dst, lhsT=lhs, rhs=sel0[:], start=True, stop=False)
-                        nc.tensor.matmul(
-                            dst,
-                            lhsT=xfix[:, HALF * pi + P * ct : HALF * pi + P * (ct + 1)],
-                            rhs=ident_b[:, 0:4],
-                            start=False,
-                            stop=True,
-                        )
-                    else:
-                        nc.tensor.matmul(dst, lhsT=lhs, rhs=selg[:], start=True, stop=True)
+        def direct(c):
+            win = slice(CHUNK * c, CHUNK * (c + 1))
+            tp = ps_aux.tile([P, CHUNK], F32, tag="aux", name="tpd%d" % c)
+            nc.tensor.matmul(tp[:], lhsT=direct_w[:, 1, :], rhs=xk[(1, 0)][:, win], start=True, stop=False)
+            nc.tensor.matmul(tp[:], lhsT=direct_w[:, 0, :], rhs=xk[(0, 0)][:, win], start=False, stop=False)
+            nc.tensor.matmul(tp[:], lhsT=direct_w[:, 2, :], rhs=x8[:, win], start=False, stop=True)
+            tps[c] = tp
 
-        def round_sums(pi):
-            nc.vector.tensor_tensor(
-                out=s1[pi][:, :, 0:36],
-                in0=sums[:, pi].rearrange("p c g q -> p q (c g)"),
-                in1=mask[:, pi],
-                op=MULT,
+        def round_direct(c):
+            tb = keep.tile([P, CHUNK], BF16, name="tb%d" % c)
+            nc.vector.tensor_tensor(out=tb[:], in0=tps[c][:], in1=m2[:, c, :], op=MULT)
+            tbs[c] = tb
+
+        def w_flip(t):
+            wt = ps_mx.tile([P, 2, P], F32, tag="acc", name="wt%d" % t)
+            words = w_sb[:, t, :].bitcast(F32).rearrange("o (p u) -> o u p", u=2)
+            for u in range(2):
+                nc.tensor.transpose(wt[:, u, :], words[:, u, :], ident_f[:])
+            wts[t] = wt
+
+        def w_copy(t):
+            nc.scalar.copy(out=gw[:, t, :, :], in_=wts[t][:].rearrange("p u o -> p o u"))
+
+        def w_quantise(t):
+            cols = slice(P * t, P * (t + 1))
+            nc.vector.quantize_mx(
+                out=w_codes[:, cols].bitcast(FP8X4),
+                scales=w_scales[:, cols],
+                in_=gw[:, t, :, :].rearrange("p o u -> p (o u)").bitcast(BF16),
             )
 
-        def flip_sums(pi):
-            pt = ps_aux.tile([P, 4, P], BF16, tag="aux", name="pt%d" % pi)
-            for q in range(4):
-                nc.tensor.transpose(pt[:, q, :], s1[pi][:, q, :], ident_b[:])
-            pts[pi] = pt
+        def sums_group8():
+            for ct in range(8):
+                nc.tensor.matmul(
+                    sums[:, :, ct // 4, 9 * (ct % 4) + 8],
+                    lhsT=x8[:, P * ct : P * (ct + 1)],
+                    rhs=sel_k[1][:, 1:4],
+                    start=True,
+                    stop=True,
+                )
 
-        def keep_flipped(pi):
-            t = keep.tile([P, 4, P], BF16, name="stt%d" % pi)
-            nc.scalar.copy(out=t[:], in_=pts[pi][:])
-            stt[pi] = t
+        def sums_quarter(q, k):
+            for ct in range(8):
+                col = 9 * (ct % 4) + 4 * k
+                nc.tensor.matmul(
+                    sums[:, q - 1, ct // 4, col : col + 4],
+                    lhsT=xk[(k, q)][:, P * ct : P * (ct + 1)],
+                    rhs=sel_k[k][:],
+                    start=True,
+                    stop=True,
+                )
+
+        def round_sums(q):
+            nc.vector.tensor_tensor(out=s1[q][:, :, 0:36], in0=sums[:, q - 1], in1=mask[:, q - 1], op=MULT)
+
+        def flip_sums(q):
+            pt = ps_aux.tile([P, 2, P], BF16, tag="aux", name="pt%d" % q)
+            for h in range(2):
+                nc.tensor.transpose(pt[:, h, :], s1[q][:, h, :], ident_b[:])
+            pts[q] = pt
+
+        def keep_flipped(q):
+            t = keep.tile([P, 2, P], BF16, name="stt%d" % q)
+            nc.scalar.copy(out=t[:], in_=pts[q][:])
+            stt[q] = t
 
         def spread_chunk(c):
             tp = ps_aux.tile([P, 4, P], BF16, tag="aux", name="tp%d" % c)
             for tl in range(4):
                 nc.tensor.matmul(
-                    tp[:, tl, :], lhsT=spread[:, tl, :], rhs=stt[c // 4][:, c % 4, :], start=True, stop=True
+                    tp[:, tl, :], lhsT=spread[:, tl, :], rhs=stt[c // 2][:, c % 2, :], start=True, stop=True
                 )
             tps[c] = tp
 
         def copy_tb(c):
-            tb = keep.tile([P, 512], BF16, name="tb%d" % c)
+            tb = keep.tile([P, CHUNK], BF16, name="tb%d" % c)
             nc.scalar.copy(out=tb[:], in_=tps[c][:].rearrange("p t n -> p (t n)"))
             tbs[c] = tb
 
         def expand(c):
-            grouped = keep.tile([P, 512, 4], BF16, name="grouped%d" % c, align_bytes=64)
-            nc.vector.tensor_copy(out=grouped[:], in_=tbs[c][:].unsqueeze(2).to_broadcast([P, 512, 4]))
+            grouped = keep.tile([P, CHUNK, 4], BF16, name="grouped%d" % c, align_bytes=64)
+            nc.vector.tensor_copy(out=grouped[:], in_=tbs[c][:].unsqueeze(2).to_broadcast([P, CHUNK, 4]))
             groupeds[c] = grouped
 
         def quantise(c):
-            cd = keep.tile([P, 512], U32, name="codes%d" % c, align_bytes=64)
-            sc = keep.tile([P, 512], U8, name="scales%d" % c, align_bytes=64)
+            cd = keep.tile([P, CHUNK], U32, name="codes%d" % c, align_bytes=64)
+            sc = keep.tile([P, CHUNK], U8, name="scales%d" % c, align_bytes=64)
             nc.vector.quantize_mx(
                 out=cd[:].bitcast(FP8X4),
                 scales=sc[:],
@@ -187,7 +254,7 @@ def tile_shiftconv_kernel(tc, x, w_pw, out):
 
         def multiply(c):
             for ot in range(4):
-                acc = ps_mx.tile([P, 512], F32, tag="acc", name="acc%d_%d" % (c, ot))
+                acc = ps_mx.tile([P, CHUNK], F32, tag="acc", name="acc%d_%d" % (c, ot))
                 nc.tensor.matmul_mx(
                     out=acc[:],
                     lhsT=w_codes[:, P * ot : P * (ot + 1)].bitcast(FP8X4),
@@ -200,42 +267,31 @@ def tile_shiftconv_kernel(tc, x, w_pw, out):
                 accs[(c, ot)] = acc
 
         def evict(c, ot, on_vector):
-            res = keep.tile([P, 512], F32, name="res%d_%d" % (c, ot))
+            res = keep.tile([P, CHUNK], F32, name="res%d_%d" % (c, ot))
             if on_vector:
                 nc.vector.tensor_copy(out=res[:], in_=accs[(c, ot)][:])
             else:
                 nc.scalar.copy(out=res[:], in_=accs[(c, ot)][:])
-            n0 = ROW * (c % 4) + HALF * (c // 4)
-            nc.sync.dma_start(out=out_v[:, ot, n0 : n0 + 512], in_=res[:])
+            nc.sync.dma_start(out=out_v[:, ot, CHUNK * c : CHUNK * (c + 1)], in_=res[:])
 
-        group_sums(0, range(NG))
-        round_sums(0)
-        flip_sums(0)
-        keep_flipped(0)
-        spread_chunk(0)
-        copy_tb(0)
-
-        gw = keep.tile([P, 4, P, 2], F32, name="gw", align_bytes=64)
-        for b in range(2):
-            wt = ps_mx.tile([P, 2, 2, P], F32, tag="acc", name="wt%d" % b)
-            for tl in range(2):
-                words = w_sb[:, 2 * b + tl, :].bitcast(F32).rearrange("o (p u) -> o u p", u=2)
-                for u in range(2):
-                    nc.tensor.transpose(wt[:, tl, u, :], words[:, u, :], ident_f[:])
-            nc.scalar.copy(out=gw[:, 2 * b : 2 * b + 2, :, :], in_=wt[:].rearrange("p t u o -> p t o u"))
-        w_codes = keep.tile([P, 512], U32, name="w_codes", align_bytes=64)
-        w_scales = keep.tile([P, 512], U8, name="w_scales", align_bytes=64)
-
+        direct(0)
+        round_direct(0)
+        direct(1)
         expand(0)
-        nc.vector.quantize_mx(
-            out=w_codes[:].bitcast(FP8X4),
-            scales=w_scales[:],
-            in_=gw[:].rearrange("p t o u -> p (t o u)").bitcast(BF16),
-        )
+        w_flip(0)
+        w_copy(0)
+        w_quantise(0)
         quantise(0)
-        spread_chunk(1)
-        copy_tb(1)
-        group_sums(1, range(0, 6))
+        for t in range(1, 4):
+            w_flip(t)
+            w_copy(t)
+        sums_group8()
+        sums_quarter(1, 0)
+        sums_quarter(1, 1)
+        for t in range(1, 4):
+            w_quantise(t)
+        round_direct(1)
+        round_sums(1)
 
         for c in range(NCHUNK):
             last = c == NCHUNK - 1
@@ -245,15 +301,35 @@ def tile_shiftconv_kernel(tc, x, w_pw, out):
                 expand(c + 1)
             evict(c, 1, True)
             evict(c, 2, False)
-            evict(c, 3, last)
-            if c + 2 < NCHUNK:
-                spread_chunk(c + 2)
-                copy_tb(c + 2)
             if c == 0:
-                group_sums(1, range(6, NG))
-            if c == 1:
-                round_sums(1)
                 flip_sums(1)
                 keep_flipped(1)
+            evict(c, 3, last)
+            if c == 0:
+                sums_quarter(2, 0)
+                sums_quarter(2, 1)
+                spread_chunk(2)
+                spread_chunk(3)
+                copy_tb(2)
+                copy_tb(3)
+                round_sums(2)
+                flip_sums(2)
+                keep_flipped(2)
+            if c == 1:
+                spread_chunk(4)
+                spread_chunk(5)
+                copy_tb(4)
+                copy_tb(5)
+                sums_quarter(3, 0)
+            if c == 2:
+                sums_quarter(3, 1)
+                round_sums(3)
+                flip_sums(3)
+                keep_flipped(3)
+            if c == 3:
+                spread_chunk(6)
+                spread_chunk(7)
+                copy_tb(6)
+                copy_tb(7)
             if not last:
                 quantise(c + 1)

@@ -13,7 +13,9 @@ U32 = mybir.dt.uint32
 FP8X4 = mybir.dt.float8_e4m3fn_x4
 ADD = mybir.AluOpType.add
 MULT = mybir.AluOpType.mult
+EQ = mybir.AluOpType.is_equal
 AX = mybir.AxisListType.X
+AXY = mybir.AxisListType.XY
 
 P = 128
 NG = 9
@@ -28,9 +30,9 @@ def shift_of(g):
 
 
 def first_channel(g):
-    if g == 0:
-        return 0
-    return 28 * g - 4
+    if g == 8:
+        return 28 * g - 4
+    return 28 * g
 
 
 def tile_shiftconv_kernel(tc, x, w_pw, out):
@@ -61,7 +63,8 @@ def tile_shiftconv_kernel(tc, x, w_pw, out):
                 nc.sync.dma_start(out=dst[g % 4 : P : 4, -b:QUARTER], in_=src[:, 0 : QUARTER + b])
             else:
                 src = x_flat[b : b + 32 * CH].rearrange("(c r) -> c r", r=CH)
-                nc.sync.dma_start(out=dst[g % 4 : P : 4, :], in_=src[:, 0:QUARTER])
+                lo = 64 if (q == 0 and g < 3) else 0
+                nc.sync.dma_start(out=dst[g % 4 : P : 4, lo:QUARTER], in_=src[:, lo:QUARTER])
 
         for g in (4, 5, 6, 7, 0, 1, 2, 3):
             load_group(g, 0)
@@ -76,18 +79,16 @@ def tile_shiftconv_kernel(tc, x, w_pw, out):
         make_identity(nc, ident_f[:])
         direct_w = keep.tile([P, 3, P], BF16, name="direct_w")
         nc.gpsimd.memset(direct_w[:], 0.0)
-        m2 = keep.tile([P, 2, CHUNK], F32, name="m2")
-        nc.gpsimd.memset(m2[:], 1.0)
+        cm = keep.tile([P, 64], F32, name="cm")
+        nc.gpsimd.memset(cm[:], 1.0)
+        ident_b = keep.tile([P, P], BF16, name="ident_b")
+        make_identity(nc, ident_b[:])
         mask = keep.tile([P, 3, 2, 36], F32, name="mask")
         nc.gpsimd.memset(mask[:], 1.0)
         s1 = {}
         for q in range(1, 4):
             s1[q] = keep.tile([P, 2, P], BF16, name="s1_%d" % q)
             nc.gpsimd.memset(s1[q][:], 0.0)
-
-        warm = keep.tile([P, 2], F32, name="warm")
-        nc.vector.memset(warm[:, 0:1], 0.0)
-        nc.scalar.copy(out=warm[:, 1:2], in_=warm[:, 0:1])
 
         selr = keep.tile([P, 2, 4], F32, name="selr")
         nc.vector.tensor_reduce(
@@ -96,52 +97,37 @@ def tile_shiftconv_kernel(tc, x, w_pw, out):
         nc.vector.tensor_reduce(
             out=selr[:, 1, :], in_=ident_f[:, 16:128].rearrange("k (c e) -> k e c", e=4), axis=AX, op=ADD
         )
-        nc.vector.tensor_copy(out=direct_w[:, 1, 56:112].rearrange("k (e r) -> k e r", r=14),
-                              in_=selr[:, 1, :].unsqueeze(2).to_broadcast([P, 4, 14]))
-        nc.vector.tensor_copy(out=direct_w[:, 1, 126:128], in_=selr[:, 1, 0:1].to_broadcast([P, 2]))
-        nc.vector.tensor_copy(out=direct_w[:, 0, 0:14], in_=selr[:, 0, 0:1].to_broadcast([P, 14]))
-        nc.vector.tensor_copy(out=direct_w[:, 0, 14:56].rearrange("k (e r) -> k e r", r=14),
-                              in_=selr[:, 1, 1:4].unsqueeze(2).to_broadcast([P, 3, 14]))
+        four = selr[:, 0, :].unsqueeze(2).to_broadcast([P, 4, 14])
+        nc.vector.tensor_copy(out=direct_w[:, 1, 56:112].rearrange("k (e r) -> k e r", r=14), in_=four)
+        nc.vector.tensor_copy(out=direct_w[:, 1, 126:128], in_=selr[:, 0, 0:1].to_broadcast([P, 2]))
+        nc.vector.tensor_copy(out=direct_w[:, 0, 0:56].rearrange("k (e r) -> k e r", r=14), in_=four)
         nc.vector.tensor_copy(out=direct_w[:, 2, 112:126], in_=selr[:, 1, 0:1].to_broadcast([P, 14]))
-
-        gm = keep.tile([P, NG], F32, name="gm")
-        nc.vector.tensor_reduce(out=gm[:], in_=ident_f[:, 0:126].rearrange("p (g r) -> p g r", r=14), axis=AX, op=ADD)
-        nc.vector.tensor_tensor(out=gm[:, 4:5], in0=gm[:, 4:5], in1=ident_f[:, 126:127], op=ADD)
-        nc.vector.tensor_tensor(out=gm[:, 4:5], in0=gm[:, 4:5], in1=ident_f[:, 127:128], op=ADD)
-        csrs = keep.tile([P, 2, 3], F32, name="csrs")
-        nc.vector.tensor_reduce(out=csrs[:, 0, :], in_=gm[:].rearrange("p (i j) -> p j i", j=3), axis=AX, op=ADD)
-        nc.vector.tensor_reduce(out=csrs[:, 1, :], in_=gm[:].rearrange("p (i j) -> p i j", j=3), axis=AX, op=ADD)
-        zz = keep.tile([P, 2, 3], F32, name="zz")
-        nc.vector.tensor_scalar(out=zz[:], in0=csrs[:], scalar1=-1.0, scalar2=1.0, op0=MULT, op1=ADD)
-        m2v = m2[:].rearrange("p a (h w) -> p (a h) w", w=64)
-        nc.vector.tensor_copy(out=m2v[:, :, 0], in_=zz[:, 0, 0:1].to_broadcast([P, 16]))
-        nc.vector.tensor_copy(out=m2v[:, :, 63], in_=zz[:, 0, 2:3].to_broadcast([P, 16]))
-        nc.vector.tensor_scalar(out=m2[:, 0, 0:64], in0=m2[:, 0, 0:64], scalar1=zz[:, 1, 0:1], scalar2=None, op0=MULT)
-
-        sel_k = []
-        for k in range(2):
-            sel_k.append(keep.tile([P, 4], BF16, name="sel_k%d" % k))
-        nc.vector.tensor_copy(out=sel_k[1][:], in_=selr[:, 1, :])
-        nc.vector.tensor_copy(out=sel_k[0][:, 0:1], in_=selr[:, 0, 0:1])
-        nc.vector.tensor_copy(out=sel_k[0][:, 1:4], in_=selr[:, 1, 1:4])
-        ident_b = keep.tile([P, P], BF16, name="ident_b")
-        nc.vector.tensor_copy(out=ident_b[:], in_=ident_f[:])
+        cs = keep.tile([P, 3], F32, name="cs")
+        nc.vector.tensor_reduce(
+            out=cs[:], in_=ident_f[:, 0:126].rearrange("p (i j r) -> p j i r", i=3, j=3), axis=AXY, op=ADD
+        )
+        nc.vector.tensor_scalar(out=cm[:, 0:64:63], in0=cs[:, 0:3:2], scalar1=0.0, scalar2=None, op0=EQ)
         ab = keep.tile([P, 2], F32, name="ab")
-        nc.vector.tensor_tensor(out=ab[:, 0:1], in0=ident_f[:, 0:1], in1=ident_f[:, 64:65], op=ADD)
-        nc.vector.tensor_tensor(out=ab[:, 1:2], in0=ident_f[:, 63:64], in1=ident_f[:, 127:128], op=ADD)
+        nc.vector.tensor_reduce(
+            out=ab[:], in_=ident_f[:].rearrange("p (h w) -> p w h", w=64)[:, 0:64:63, :], axis=AX, op=ADD
+        )
         nab = keep.tile([P, 2], F32, name="nab")
-        nc.vector.tensor_scalar(out=nab[:], in0=ab[:], scalar1=-1.0, scalar2=1.0, op0=MULT, op1=ADD)
+        nc.vector.tensor_scalar(out=nab[:], in0=ab[:], scalar1=0.0, scalar2=None, op0=EQ)
+
+        sel_k = keep.tile([P, 4], BF16, name="sel_k")
+        nc.scalar.copy(out=sel_k[:], in_=selr[:, 0, :])
+        sel_8 = keep.tile([P, 4], BF16, name="sel_8")
+        nc.scalar.copy(out=sel_8[:], in_=selr[:, 1, :])
         mv = mask[:].rearrange("p a h (c i j) -> p (a h c i) j", i=3, j=3)
-        nc.vector.tensor_copy(out=mv[:, :, 0], in_=nab[:, 0:1].to_broadcast([P, 72]))
-        nc.vector.tensor_copy(out=mv[:, :, 2], in_=nab[:, 1:2].to_broadcast([P, 72]))
-        nc.vector.memset(mask[64:128, 2, 1, 33:36], 0.0)
+        nc.scalar.copy(out=mv[:, :, 0:3:2], in_=nab[:].unsqueeze(1).to_broadcast([P, 72, 2]))
+        nc.gpsimd.memset(mask[64:128, 2, 1, 33:36], 0.0)
         spread = keep.tile([P, 4, P], BF16, name="spread")
-        idg = ident_f[:, 0:36].rearrange("k (t g) -> k t g", g=NG)
-        nc.vector.tensor_copy(
+        idg = ident_b[:, 0:36].rearrange("k (t g) -> k t g", g=NG)
+        nc.scalar.copy(
             out=spread[:, :, 0:126].rearrange("k t (g r) -> k t g r", r=14),
             in_=idg.unsqueeze(3).to_broadcast([P, 4, NG, 14]),
         )
-        nc.vector.tensor_copy(out=spread[:, :, 126:128], in_=idg[:, :, 4:5].to_broadcast([P, 4, 2]))
+        nc.scalar.copy(out=spread[:, :, 126:128], in_=idg[:, :, 4:5].to_broadcast([P, 4, 2]))
 
         sums = ps_sum.tile([P, 3, 2, 36], F32, name="sums")
         gw = keep.tile([P, 4, P, 2], F32, name="gw", align_bytes=64)
@@ -167,7 +153,12 @@ def tile_shiftconv_kernel(tc, x, w_pw, out):
 
         def round_direct(c):
             tb = keep.tile([P, CHUNK], BF16, name="tb%d" % c)
-            nc.vector.tensor_tensor(out=tb[:], in0=tps[c][:], in1=m2[:, c, :], op=MULT)
+            nc.vector.tensor_tensor(
+                out=tb[:].rearrange("p (h w) -> p h w", w=64),
+                in0=tps[c][:].rearrange("p (h w) -> p h w", w=64),
+                in1=cm[:].unsqueeze(1).to_broadcast([P, 8, 64]),
+                op=MULT,
+            )
             tbs[c] = tb
 
         def w_flip(t):
@@ -193,7 +184,7 @@ def tile_shiftconv_kernel(tc, x, w_pw, out):
                 nc.tensor.matmul(
                     sums[:, :, ct // 4, 9 * (ct % 4) + 8],
                     lhsT=x8[:, P * ct : P * (ct + 1)],
-                    rhs=sel_k[1][:, 1:4],
+                    rhs=sel_8[:, 1:4],
                     start=True,
                     stop=True,
                 )
@@ -204,7 +195,7 @@ def tile_shiftconv_kernel(tc, x, w_pw, out):
                 nc.tensor.matmul(
                     sums[:, q - 1, ct // 4, col : col + 4],
                     lhsT=xk[(k, q)][:, P * ct : P * (ct + 1)],
-                    rhs=sel_k[k][:],
+                    rhs=sel_k[:],
                     start=True,
                     stop=True,
                 )
@@ -290,8 +281,8 @@ def tile_shiftconv_kernel(tc, x, w_pw, out):
         sums_quarter(1, 1)
         for t in range(1, 4):
             w_quantise(t)
-        round_direct(1)
         round_sums(1)
+        round_direct(1)
 
         for c in range(NCHUNK):
             last = c == NCHUNK - 1
@@ -299,7 +290,7 @@ def tile_shiftconv_kernel(tc, x, w_pw, out):
             evict(c, 0, False)
             if not last:
                 expand(c + 1)
-            evict(c, 1, True)
+            evict(c, 1, c > 0)
             evict(c, 2, False)
             if c == 0:
                 flip_sums(1)

@@ -14,6 +14,7 @@ FP8X4 = mybir.dt.float8_e4m3fn_x4
 ADD = mybir.AluOpType.add
 MULT = mybir.AluOpType.mult
 EQ = mybir.AluOpType.is_equal
+COPY = mybir.ActivationFunctionType.Copy
 AX = mybir.AxisListType.X
 AXY = mybir.AxisListType.XY
 
@@ -161,6 +162,14 @@ def tile_shiftconv_kernel(tc, x, w_pw, out):
             )
             tbs[c] = tb
 
+        def round_direct_on_scalar(c):
+            tb = keep.tile([P, CHUNK], BF16, name="tb%d" % c)
+            nc.scalar.copy(out=tb[:], in_=tps[c][:])
+            tbv = tb[:].rearrange("p (h w) -> p h w", w=64)
+            for col in (0, 63):
+                nc.scalar.activation(out=tbv[:, :, col], in_=tbv[:, :, col], func=COPY, scale=cm[:, col : col + 1])
+            tbs[c] = tb
+
         def w_flip(t):
             wt = ps_mx.tile([P, 2, P], F32, tag="acc", name="wt%d" % t)
             words = w_sb[:, t, :].bitcast(F32).rearrange("o (p u) -> o u p", u=2)
@@ -276,51 +285,50 @@ def tile_shiftconv_kernel(tc, x, w_pw, out):
         for t in range(1, 4):
             w_flip(t)
             w_copy(t)
+        round_direct_on_scalar(1)
         sums_group8()
         sums_quarter(1, 0)
         sums_quarter(1, 1)
         for t in range(1, 4):
             w_quantise(t)
         round_sums(1)
-        round_direct(1)
 
         for c in range(NCHUNK):
             last = c == NCHUNK - 1
+            helps = c in (2, 4, 5, 6, 7)
             multiply(c)
             evict(c, 0, False)
             if not last:
                 expand(c + 1)
-            evict(c, 1, c > 0)
-            evict(c, 2, False)
             if c == 0:
                 flip_sums(1)
                 keep_flipped(1)
-            evict(c, 3, last)
+            evict(c, 1, helps)
             if c == 0:
                 sums_quarter(2, 0)
-                sums_quarter(2, 1)
                 spread_chunk(2)
-                spread_chunk(3)
                 copy_tb(2)
+            if c in (1, 3):
+                q = (c + 3) // 2
+                round_sums(q)
+                flip_sums(q)
+                keep_flipped(q)
+                if c == 1:
+                    sums_quarter(3, 0)
+                spread_chunk(2 * q)
+            evict(c, 2, False)
+            if c == 0:
+                spread_chunk(3)
                 copy_tb(3)
-                round_sums(2)
-                flip_sums(2)
-                keep_flipped(2)
-            if c == 1:
-                spread_chunk(4)
-                spread_chunk(5)
-                copy_tb(4)
-                copy_tb(5)
-                sums_quarter(3, 0)
+            if c in (2, 4):
+                spread_chunk(c + 3)
+                copy_tb(c + 3)
+            evict(c, 3, last)
+            if c == 0:
+                sums_quarter(2, 1)
+            if c in (1, 3):
+                copy_tb(c + 3)
             if c == 2:
                 sums_quarter(3, 1)
-                round_sums(3)
-                flip_sums(3)
-                keep_flipped(3)
-            if c == 3:
-                spread_chunk(6)
-                spread_chunk(7)
-                copy_tb(6)
-                copy_tb(7)
             if not last:
                 quantise(c + 1)

@@ -55,13 +55,18 @@ def tile_shiftconv_kernel(tc, x, w_pw, out):
         x8 = keep.tile([P, QUARTER], BF16, name="x8")
         w_sb = keep.tile([P, 4, 512], BF16, name="w_sb")
         nc.vector.memset(xk[(0, 0)][:, 0:80].bitcast(I32), 0)
+        head0 = keep.tile([P, 16], BF16, name="head0")
 
         def load_group(g, q):
             dst = xk[(g // 4, q)]
             b = first_channel(g) * CH + QUARTER * q + shift_of(g)
             if b < 0:
-                src = x_flat[0 : 32 * CH].rearrange("(c r) -> c r", r=CH)
-                nc.sync.dma_start(out=dst[g % 4 : P : 4, -b:QUARTER], in_=src[:, 0 : QUARTER + b])
+                src = x_flat[CH + b : 32 * CH + b].rearrange("(c r) -> c r", r=CH)
+                nc.sync.dma_start(out=dst[4:P:4, 64:QUARTER], in_=src[:, 64:QUARTER])
+                nc.sync.dma_start(out=head0[0:1, :], in_=x_flat[0:16].rearrange("(r l) -> r l", l=16))
+                nc.sync.dma_start(
+                    out=dst[0:1, 80:QUARTER], in_=x_flat[80 + b : QUARTER + b].rearrange("(r l) -> r l", l=QUARTER - 80)
+                )
             else:
                 src = x_flat[b : b + 32 * CH].rearrange("(c r) -> c r", r=CH)
                 lo = 64 if (q == 0 and g < 3) else 0
@@ -114,6 +119,7 @@ def tile_shiftconv_kernel(tc, x, w_pw, out):
         )
         nab = keep.tile([P, 2], F32, name="nab")
         nc.vector.tensor_scalar(out=nab[:], in0=ab[:], scalar1=0.0, scalar2=None, op0=EQ)
+        nc.vector.tensor_copy(out=xk[(0, 0)][0:1, 65:80], in_=head0[0:1, 0:15])
 
         sel_k = keep.tile([P, 4], BF16, name="sel_k")
         nc.scalar.copy(out=sel_k[:], in_=selr[:, 0, :])

@@ -24,6 +24,7 @@ CH = 4096
 QUARTER = 1024
 CHUNK = 512
 NCHUNK = 8
+W0 = QUARTER + 64
 
 
 def shift_of(g):
@@ -48,42 +49,47 @@ def tile_shiftconv_kernel(tc, x, w_pw, out):
         x_flat = x.rearrange("b c h w -> (b c h w)")
         out_v = out.rearrange("b (o t) h w -> o (b t) (h w)", t=4)
 
+        xt0 = keep.tile([P, 64 + 3 * W0], BF16, name="xt0")
+        blocks = xt0[:, 64 : 64 + 3 * W0].rearrange("p (i m) -> p i m", i=3)
+        head = keep.tile([P, 3, 16], BF16, name="head")
         xk = {}
-        for q in range(4):
+        for q in range(1, 4):
             for k in range(2):
                 xk[(k, q)] = keep.tile([P, QUARTER], BF16, name="xk%d_%d" % (k, q))
         x8 = keep.tile([P, QUARTER], BF16, name="x8")
         w_sb = keep.tile([P, 4, 512], BF16, name="w_sb")
-        nc.vector.memset(xk[(0, 0)][:, 0:80].bitcast(I32), 0)
-        head0 = keep.tile([P, 16], BF16, name="head0")
+        nc.vector.memset(head[:].bitcast(I32), 0)
+        nc.vector.memset(xt0[:, 0:80].bitcast(I32), 0)
+        nc.vector.memset(blocks[:, 1:3, 0:16].bitcast(I32), 0)
+
+        def channel_rows(shift):
+            return x_flat[shift : shift + 252 * CH].rearrange("(i r c) -> r i c", i=3, r=84)
+
+        def load_first_quarter(lo, hi):
+            nc.sync.dma_start(out=blocks[1:P:2, :, lo:hi], in_=channel_rows(0)[20:84, :, lo:hi])
+            nc.sync.dma_start(out=blocks[2:P:4, :, lo:hi], in_=channel_rows(1)[52:84, :, lo:hi])
+            first = max(lo, 16)
+            nc.sync.dma_start(out=blocks[0:P:4, :, first:hi], in_=channel_rows(15)[0:32, :, first - 16 : hi - 16])
 
         def load_group(g, q):
             dst = xk[(g // 4, q)]
             b = first_channel(g) * CH + QUARTER * q + shift_of(g)
-            if b < 0:
-                src = x_flat[CH + b : 32 * CH + b].rearrange("(c r) -> c r", r=CH)
-                nc.sync.dma_start(out=dst[4:P:4, 64:QUARTER], in_=src[:, 64:QUARTER])
-                nc.sync.dma_start(out=head0[0:1, :], in_=x_flat[0:16].rearrange("(r l) -> r l", l=16))
-                nc.sync.dma_start(
-                    out=dst[0:1, 80:QUARTER], in_=x_flat[80 + b : QUARTER + b].rearrange("(r l) -> r l", l=QUARTER - 80)
-                )
-            else:
-                src = x_flat[b : b + 32 * CH].rearrange("(c r) -> c r", r=CH)
-                lo = 64 if (q == 0 and g < 3) else 0
-                nc.sync.dma_start(out=dst[g % 4 : P : 4, lo:QUARTER], in_=src[:, lo:QUARTER])
+            src = x_flat[b : b + 32 * CH].rearrange("(c r) -> c r", r=CH)
+            nc.sync.dma_start(out=dst[g % 4 : P : 4, :], in_=src[:, 0:QUARTER])
 
-        for g in (4, 5, 6, 7, 0, 1, 2, 3):
-            load_group(g, 0)
+        nc.sync.dma_start(out=head[0:P:4, :, :], in_=channel_rows(0)[0:32, :, 0:16])
+        load_first_quarter(0, CHUNK + 64)
+        nc.sync.dma_start(out=w_sb[:], in_=w_pw.rearrange("(o t) c -> o t c", t=4))
+        load_first_quarter(CHUNK + 64, W0)
         b8 = first_channel(8) * CH + shift_of(8)
         nc.sync.dma_start(out=x8[:], in_=x_flat[b8 : b8 + P * QUARTER].rearrange("(r l) -> r l", l=QUARTER))
-        nc.sync.dma_start(out=w_sb[:], in_=w_pw.rearrange("(o t) c -> o t c", t=4))
         for q in range(1, 4):
             for g in range(8):
                 load_group(g, q)
 
         ident_f = keep.tile([P, P], F32, name="ident_f")
         make_identity(nc, ident_f[:])
-        direct_w = keep.tile([P, 3, P], BF16, name="direct_w")
+        direct_w = keep.tile([P, 4 * P], BF16, name="direct_w")
         nc.gpsimd.memset(direct_w[:], 0.0)
         cm = keep.tile([P, 64], F32, name="cm")
         nc.gpsimd.memset(cm[:], 1.0)
@@ -103,11 +109,16 @@ def tile_shiftconv_kernel(tc, x, w_pw, out):
         nc.vector.tensor_reduce(
             out=selr[:, 1, :], in_=ident_f[:, 16:128].rearrange("k (c e) -> k e c", e=4), axis=AX, op=ADD
         )
-        four = selr[:, 0, :].unsqueeze(2).to_broadcast([P, 4, 14])
-        nc.vector.tensor_copy(out=direct_w[:, 1, 56:112].rearrange("k (e r) -> k e r", r=14), in_=four)
-        nc.vector.tensor_copy(out=direct_w[:, 1, 126:128], in_=selr[:, 0, 0:1].to_broadcast([P, 2]))
-        nc.vector.tensor_copy(out=direct_w[:, 0, 0:56].rearrange("k (e r) -> k e r", r=14), in_=four)
-        nc.vector.tensor_copy(out=direct_w[:, 2, 112:126], in_=selr[:, 1, 0:1].to_broadcast([P, 14]))
+        sel_odd = keep.tile([P, 2], F32, name="sel_odd")
+        nc.vector.tensor_reduce(
+            out=sel_odd[:], in_=ident_f[:, 16:72].rearrange("k (c e) -> k e c", e=2), axis=AX, op=ADD
+        )
+        diagonal = direct_w[:, 0:510].rearrange("k (i z) -> k i z", z=170)
+        for j, rows_of_j in ((0, selr[:, 0, 0:1]), (1, sel_odd[:, 1:2]), (2, selr[:, 1, 2:3])):
+            nc.vector.tensor_copy(
+                out=diagonal[:, :, 14 * j : 14 * j + 14], in_=rows_of_j.unsqueeze(2).to_broadcast([P, 3, 14])
+            )
+        nc.vector.tensor_copy(out=direct_w[:, P + 126 : P + 128], in_=sel_odd[:, 1:2].to_broadcast([P, 2]))
         cs = keep.tile([P, 3], F32, name="cs")
         nc.vector.tensor_reduce(
             out=cs[:], in_=ident_f[:, 0:126].rearrange("p (i j r) -> p j i r", i=3, j=3), axis=AXY, op=ADD
@@ -119,7 +130,7 @@ def tile_shiftconv_kernel(tc, x, w_pw, out):
         )
         nab = keep.tile([P, 2], F32, name="nab")
         nc.vector.tensor_scalar(out=nab[:], in0=ab[:], scalar1=0.0, scalar2=None, op0=EQ)
-        nc.vector.tensor_copy(out=xk[(0, 0)][0:1, 65:80], in_=head0[0:1, 0:15])
+        nc.vector.tensor_tensor(out=blocks[:, :, 1:16], in0=blocks[:, :, 1:16], in1=head[:, :, 0:15], op=ADD)
 
         sel_k = keep.tile([P, 4], BF16, name="sel_k")
         nc.scalar.copy(out=sel_k[:], in_=selr[:, 0, :])
@@ -151,11 +162,12 @@ def tile_shiftconv_kernel(tc, x, w_pw, out):
         accs = {}
 
         def direct(c):
-            win = slice(CHUNK * c, CHUNK * (c + 1))
             tp = ps_aux.tile([P, CHUNK], F32, tag="aux", name="tpd%d" % c)
-            nc.tensor.matmul(tp[:], lhsT=direct_w[:, 1, :], rhs=xk[(1, 0)][:, win], start=True, stop=False)
-            nc.tensor.matmul(tp[:], lhsT=direct_w[:, 0, :], rhs=xk[(0, 0)][:, win], start=False, stop=False)
-            nc.tensor.matmul(tp[:], lhsT=direct_w[:, 2, :], rhs=x8[:, win], start=False, stop=True)
+            for i in range(3):
+                lo = W0 * i + CHUNK * c + 64 * i
+                nc.tensor.matmul(
+                    tp[:], lhsT=direct_w[:, P * i : P * (i + 1)], rhs=xt0[:, lo : lo + CHUNK], start=i == 0, stop=i == 2
+                )
             tps[c] = tp
 
         def round_direct(c):
@@ -282,15 +294,15 @@ def tile_shiftconv_kernel(tc, x, w_pw, out):
 
         direct(0)
         round_direct(0)
-        direct(1)
-        expand(0)
         w_flip(0)
         w_copy(0)
+        expand(0)
         w_quantise(0)
         quantise(0)
         for t in range(1, 4):
             w_flip(t)
             w_copy(t)
+        direct(1)
         round_direct_on_scalar(1)
         sums_group8()
         sums_quarter(1, 0)

@@ -25,6 +25,7 @@ QUARTER = 1024
 CHUNK = 512
 NCHUNK = 8
 W0 = QUARTER + 64
+PAIR_FIRST = (0, 1, 4, 5)
 
 
 def shift_of(g):
@@ -52,10 +53,7 @@ def tile_shiftconv_kernel(tc, x, w_pw, out):
         xt0 = keep.tile([P, 64 + 3 * W0], BF16, name="xt0")
         blocks = xt0[:, 64 : 64 + 3 * W0].rearrange("p (i m) -> p i m", i=3)
         head = keep.tile([P, 3, 16], BF16, name="head")
-        xk = {}
-        for q in range(1, 4):
-            for k in range(2):
-                xk[(k, q)] = keep.tile([P, QUARTER], BF16, name="xk%d_%d" % (k, q))
+        xq = keep.tile([P, 2, 3 * QUARTER], BF16, name="xq")
         x8 = keep.tile([P, QUARTER], BF16, name="x8")
         w_sb = keep.tile([P, 4, 512], BF16, name="w_sb")
         nc.vector.memset(head[:].bitcast(I32), 0)
@@ -71,11 +69,12 @@ def tile_shiftconv_kernel(tc, x, w_pw, out):
             first = max(lo, 16)
             nc.sync.dma_start(out=blocks[0:P:4, :, first:hi], in_=channel_rows(15)[0:32, :, first - 16 : hi - 16])
 
-        def load_group(g, q):
-            dst = xk[(g // 4, q)]
-            b = first_channel(g) * CH + QUARTER * q + shift_of(g)
-            src = x_flat[b : b + 32 * CH].rearrange("(c r) -> c r", r=CH)
-            nc.sync.dma_start(out=dst[g % 4 : P : 4, :], in_=src[:, 0:QUARTER])
+        def load_pair(e, lo, hi):
+            g = PAIR_FIRST[e]
+            b = first_channel(g) * CH + QUARTER + shift_of(g)
+            apart = 56 * CH + shift_of(g + 2) - shift_of(g)
+            both = x_flat[b : b + 2 * apart].rearrange("(k z) -> k z", k=2)[:, 0 : 32 * CH]
+            nc.sync.dma_start(out=xq[e:P:4, :, lo:hi], in_=both.rearrange("k (r c) -> r k c", c=CH)[:, :, lo:hi])
 
         nc.sync.dma_start(out=head[0:P:4, :, :], in_=channel_rows(0)[0:32, :, 0:16])
         load_first_quarter(0, CHUNK + 64)
@@ -83,9 +82,10 @@ def tile_shiftconv_kernel(tc, x, w_pw, out):
         load_first_quarter(CHUNK + 64, W0)
         b8 = first_channel(8) * CH + shift_of(8)
         nc.sync.dma_start(out=x8[:], in_=x_flat[b8 : b8 + P * QUARTER].rearrange("(r l) -> r l", l=QUARTER))
-        for q in range(1, 4):
-            for g in range(8):
-                load_group(g, q)
+        for e in range(4):
+            load_pair(e, 0, QUARTER)
+        for e in range(4):
+            load_pair(e, QUARTER, 3 * QUARTER)
 
         ident_f = keep.tile([P, P], F32, name="ident_f")
         make_identity(nc, ident_f[:])
@@ -147,7 +147,8 @@ def tile_shiftconv_kernel(tc, x, w_pw, out):
         )
         nc.scalar.copy(out=spread[:, :, 126:128], in_=idg[:, :, 4:5].to_broadcast([P, 4, 2]))
 
-        sums = ps_sum.tile([P, 3, 2, 36], F32, name="sums")
+        sums_flat = ps_sum.tile([P, 224], F32, name="sums")
+        sums = sums_flat[:, 0:216].rearrange("p (q h c) -> p q h c", q=3, h=2)
         gw = keep.tile([P, 4, P, 2], F32, name="gw", align_bytes=64)
         w_codes = keep.tile([P, 512], U32, name="w_codes", align_bytes=64)
         w_scales = keep.tile([P, 512], U8, name="w_scales", align_bytes=64)
@@ -218,11 +219,12 @@ def tile_shiftconv_kernel(tc, x, w_pw, out):
 
         def sums_quarter(q, k):
             for ct in range(8):
-                col = 9 * (ct % 4) + 4 * k
+                col = 72 * (q - 1) + 36 * (ct // 4) + 9 * (ct % 4) + 2 * k
+                first = QUARTER * (q - 1) + P * ct
                 nc.tensor.matmul(
-                    sums[:, q - 1, ct // 4, col : col + 4],
-                    lhsT=xk[(k, q)][:, P * ct : P * (ct + 1)],
-                    rhs=sel_k[:],
+                    sums_flat[:, col : col + 8].rearrange("p (a b) -> p a b", b=4)[:, :, 0:2],
+                    lhsT=xq[:, k, first : first + P],
+                    rhs=sel_k[:].rearrange("p (a b) -> p a b", b=2),
                     start=True,
                     stop=True,
                 )

@@ -24,12 +24,22 @@ CH = 4096
 QUARTER = 1024
 CHUNK = 512
 NCHUNK = 8
+TWO_ONES = 0x3F803F80
+HALF = 256
 W0 = QUARTER + 64
 PAIR_FIRST = (0, 1, 4, 5)
 
 
 def shift_of(g):
     return 64 * (g // 3 - 1) + (g % 3 - 1)
+
+
+def span(piece):
+    if piece == "a":
+        return 0, HALF
+    if piece == "b":
+        return HALF, HALF
+    return CHUNK * piece, CHUNK
 
 
 def first_channel(g):
@@ -47,6 +57,23 @@ def tile_shiftconv_kernel(tc, x, w_pw, out):
         ps_mx = ctx.enter_context(tc.psum_pool(name="ps_mx", bufs=5))
         ctx.enter_context(tc.manual_schedule())
 
+        warm_in = keep.tile([P, 512], BF16, name="warm_in", align_bytes=64)
+        warm_codes = keep.tile([P, P], U32, name="warm_codes", align_bytes=64)
+        warm_scales = keep.tile([P, P], U8, name="warm_scales", align_bytes=64)
+        nc.vector.memset(warm_in[:].bitcast(I32), TWO_ONES)
+        nc.vector.quantize_mx(out=warm_codes[:].bitcast(FP8X4), scales=warm_scales[:], in_=warm_in[:])
+        idle = ps_mx.tile([P, 4, P], F32, tag="acc", name="idle")
+        for k in range(11):
+            nc.tensor.matmul_mx(
+                out=idle[:, k % 4, :],
+                lhsT=warm_codes[:].bitcast(FP8X4),
+                lhsT_scale=warm_scales[:],
+                rhs=warm_codes[:].bitcast(FP8X4),
+                rhs_scale=warm_scales[:],
+                start=True,
+                stop=True,
+            )
+
         x_flat = x.rearrange("b c h w -> (b c h w)")
         out_v = out.rearrange("b (o t) h w -> o (b t) (h w)", t=4)
 
@@ -56,9 +83,9 @@ def tile_shiftconv_kernel(tc, x, w_pw, out):
         xq = keep.tile([P, 2, 3 * QUARTER], BF16, name="xq")
         x8 = keep.tile([P, QUARTER], BF16, name="x8")
         w_sb = keep.tile([P, 4, 512], BF16, name="w_sb")
-        nc.vector.memset(head[:].bitcast(I32), 0)
-        nc.vector.memset(xt0[:, 0:80].bitcast(I32), 0)
-        nc.vector.memset(blocks[:, 1:3, 0:16].bitcast(I32), 0)
+        nc.gpsimd.memset(head[:], 0.0)
+        nc.gpsimd.memset(xt0[:, 0:80], 0.0)
+        nc.gpsimd.memset(blocks[:, 1:3, 0:16], 0.0)
 
         def channel_rows(shift):
             return x_flat[shift : shift + 252 * CH].rearrange("(i r c) -> r i c", i=3, r=84)
@@ -77,8 +104,9 @@ def tile_shiftconv_kernel(tc, x, w_pw, out):
             nc.sync.dma_start(out=xq[e:P:4, :, lo:hi], in_=both.rearrange("k (r c) -> r k c", c=CH)[:, :, lo:hi])
 
         nc.sync.dma_start(out=head[0:P:4, :, :], in_=channel_rows(0)[0:32, :, 0:16])
-        load_first_quarter(0, CHUNK + 64)
+        load_first_quarter(0, HALF + 64)
         nc.sync.dma_start(out=w_sb[:], in_=w_pw.rearrange("(o t) c -> o t c", t=4))
+        load_first_quarter(HALF + 64, CHUNK + 64)
         load_first_quarter(CHUNK + 64, W0)
         b8 = first_channel(8) * CH + shift_of(8)
         nc.sync.dma_start(out=x8[:], in_=x_flat[b8 : b8 + P * QUARTER].rearrange("(r l) -> r l", l=QUARTER))
@@ -147,6 +175,7 @@ def tile_shiftconv_kernel(tc, x, w_pw, out):
         )
         nc.scalar.copy(out=spread[:, :, 126:128], in_=idg[:, :, 4:5].to_broadcast([P, 4, 2]))
 
+
         sums_flat = ps_sum.tile([P, 224], F32, name="sums")
         sums = sums_flat[:, 0:216].rearrange("p (q h c) -> p q h c", q=3, h=2)
         gw = keep.tile([P, 4, P, 2], F32, name="gw", align_bytes=64)
@@ -162,32 +191,35 @@ def tile_shiftconv_kernel(tc, x, w_pw, out):
         scales = {}
         accs = {}
 
-        def direct(c):
-            tp = ps_aux.tile([P, CHUNK], F32, tag="aux", name="tpd%d" % c)
+        def direct(piece):
+            first, n = span(piece)
+            tp = ps_aux.tile([P, CHUNK], F32, tag="aux", name="tpd%s" % piece)
             for i in range(3):
-                lo = W0 * i + CHUNK * c + 64 * i
+                lo = W0 * i + first + 64 * i
                 nc.tensor.matmul(
-                    tp[:], lhsT=direct_w[:, P * i : P * (i + 1)], rhs=xt0[:, lo : lo + CHUNK], start=i == 0, stop=i == 2
+                    tp[:, 0:n], lhsT=direct_w[:, P * i : P * (i + 1)], rhs=xt0[:, lo : lo + n], start=i == 0, stop=i == 2
                 )
-            tps[c] = tp
+            tps[piece] = tp
 
-        def round_direct(c):
-            tb = keep.tile([P, CHUNK], BF16, name="tb%d" % c)
+        def round_direct(piece):
+            n = span(piece)[1]
+            tb = keep.tile([P, n], BF16, name="tb%s" % piece)
             nc.vector.tensor_tensor(
                 out=tb[:].rearrange("p (h w) -> p h w", w=64),
-                in0=tps[c][:].rearrange("p (h w) -> p h w", w=64),
-                in1=cm[:].unsqueeze(1).to_broadcast([P, 8, 64]),
+                in0=tps[piece][:, 0:n].rearrange("p (h w) -> p h w", w=64),
+                in1=cm[:].unsqueeze(1).to_broadcast([P, n // 64, 64]),
                 op=MULT,
             )
-            tbs[c] = tb
+            tbs[piece] = tb
 
-        def round_direct_on_scalar(c):
-            tb = keep.tile([P, CHUNK], BF16, name="tb%d" % c)
-            nc.scalar.copy(out=tb[:], in_=tps[c][:])
+        def round_direct_on_scalar(piece):
+            n = span(piece)[1]
+            tb = keep.tile([P, n], BF16, name="tb%s" % piece)
+            nc.scalar.copy(out=tb[:], in_=tps[piece][:, 0:n])
             tbv = tb[:].rearrange("p (h w) -> p h w", w=64)
             for col in (0, 63):
                 nc.scalar.activation(out=tbv[:, :, col], in_=tbv[:, :, col], func=COPY, scale=cm[:, col : col + 1])
-            tbs[c] = tb
+            tbs[piece] = tb
 
         def w_flip(t):
             wt = ps_mx.tile([P, 2, P], F32, tag="acc", name="wt%d" % t)
@@ -256,78 +288,107 @@ def tile_shiftconv_kernel(tc, x, w_pw, out):
             nc.scalar.copy(out=tb[:], in_=tps[c][:].rearrange("p t n -> p (t n)"))
             tbs[c] = tb
 
-        def expand(c):
-            grouped = keep.tile([P, CHUNK, 4], BF16, name="grouped%d" % c, align_bytes=64)
-            nc.vector.tensor_copy(out=grouped[:], in_=tbs[c][:].unsqueeze(2).to_broadcast([P, CHUNK, 4]))
-            groupeds[c] = grouped
+        def expand(piece):
+            n = span(piece)[1]
+            grouped = keep.tile([P, n, 4], BF16, name="grouped%s" % piece, align_bytes=64)
+            nc.vector.tensor_copy(out=grouped[:], in_=tbs[piece][:].unsqueeze(2).to_broadcast([P, n, 4]))
+            groupeds[piece] = grouped
 
-        def quantise(c):
-            cd = keep.tile([P, CHUNK], U32, name="codes%d" % c, align_bytes=64)
-            sc = keep.tile([P, CHUNK], U8, name="scales%d" % c, align_bytes=64)
+        def quantise(piece):
+            n = span(piece)[1]
+            cd = keep.tile([P, n], U32, name="codes%s" % piece, align_bytes=64)
+            sc = keep.tile([P, n], U8, name="scales%s" % piece, align_bytes=64)
             nc.vector.quantize_mx(
                 out=cd[:].bitcast(FP8X4),
                 scales=sc[:],
-                in_=groupeds[c][:].rearrange("p n j -> p (n j)"),
+                in_=groupeds[piece][:].rearrange("p n j -> p (n j)"),
             )
-            codes[c] = cd
-            scales[c] = sc
+            codes[piece] = cd
+            scales[piece] = sc
 
-        def multiply(c):
-            for ot in range(4):
-                acc = ps_mx.tile([P, CHUNK], F32, tag="acc", name="acc%d_%d" % (c, ot))
+        def multiply_bank(piece, bank):
+            n = span(piece)[1]
+            per_bank = CHUNK // n
+            acc = ps_mx.tile([P, per_bank, n], F32, tag="acc", name="acc%s_%d" % (piece, bank))
+            accs[(piece, bank)] = acc
+            for k in range(per_bank):
+                ot = per_bank * bank + k
                 nc.tensor.matmul_mx(
-                    out=acc[:],
+                    out=acc[:, k, :],
                     lhsT=w_codes[:, P * ot : P * (ot + 1)].bitcast(FP8X4),
                     lhsT_scale=w_scales[:, P * ot : P * (ot + 1)],
-                    rhs=codes[c][:].bitcast(FP8X4),
-                    rhs_scale=scales[c][:],
+                    rhs=codes[piece][:].bitcast(FP8X4),
+                    rhs_scale=scales[piece][:],
                     start=True,
                     stop=True,
                 )
-                accs[(c, ot)] = acc
 
-        def evict(c, ot, on_vector):
-            res = keep.tile([P, CHUNK], F32, name="res%d_%d" % (c, ot))
+        def multiply(piece):
+            for bank in range(4 * span(piece)[1] // CHUNK):
+                multiply_bank(piece, bank)
+
+        def evict(piece, bank, on_vector):
+            first, n = span(piece)
+            per_bank = CHUNK // n
+            res = keep.tile([P, per_bank, n], F32, name="res%s_%d" % (piece, bank))
             if on_vector:
-                nc.vector.tensor_copy(out=res[:], in_=accs[(c, ot)][:])
+                nc.vector.tensor_copy(out=res[:], in_=accs[(piece, bank)][:])
             else:
-                nc.scalar.copy(out=res[:], in_=accs[(c, ot)][:])
-            nc.sync.dma_start(out=out_v[:, ot, CHUNK * c : CHUNK * (c + 1)], in_=res[:])
+                nc.scalar.copy(out=res[:], in_=accs[(piece, bank)][:])
+            nc.sync.dma_start(out=out_v[:, per_bank * bank : per_bank * (bank + 1), first : first + n], in_=res[:])
 
-        direct(0)
-        round_direct(0)
+        direct("a")
+        round_direct("a")
         w_flip(0)
         w_copy(0)
-        expand(0)
+        expand("a")
+        w_flip(1)
+        w_copy(1)
+        direct("b")
         w_quantise(0)
-        quantise(0)
-        for t in range(1, 4):
-            w_flip(t)
-            w_copy(t)
+        quantise("a")
+        w_quantise(1)
+        round_direct("b")
+        w_flip(2)
+        w_copy(2)
+        w_flip(3)
+        w_copy(3)
         direct(1)
         round_direct_on_scalar(1)
+        multiply_bank("a", 0)
+        expand("b")
         sums_group8()
         sums_quarter(1, 0)
         sums_quarter(1, 1)
-        for t in range(1, 4):
-            w_quantise(t)
+        w_quantise(2)
+        w_quantise(3)
+        evict("a", 0, False)
+        multiply_bank("a", 1)
+        quantise("b")
         round_sums(1)
+        flip_sums(1)
+        keep_flipped(1)
+        evict("a", 1, False)
+        multiply("b")
+        expand(1)
+        spread_chunk(2)
+        copy_tb(2)
+        evict("b", 0, False)
+        sums_quarter(2, 0)
+        quantise(1)
+        spread_chunk(3)
+        evict("b", 1, False)
+        copy_tb(3)
+        sums_quarter(2, 1)
 
-        for c in range(NCHUNK):
+        for c in range(1, NCHUNK):
             last = c == NCHUNK - 1
             helps = c in (2, 4, 5, 6, 7)
             multiply(c)
             evict(c, 0, False)
             if not last:
                 expand(c + 1)
-            if c == 0:
-                flip_sums(1)
-                keep_flipped(1)
             evict(c, 1, helps)
-            if c == 0:
-                sums_quarter(2, 0)
-                spread_chunk(2)
-                copy_tb(2)
             if c in (1, 3):
                 q = (c + 3) // 2
                 round_sums(q)
@@ -337,15 +398,10 @@ def tile_shiftconv_kernel(tc, x, w_pw, out):
                     sums_quarter(3, 0)
                 spread_chunk(2 * q)
             evict(c, 2, False)
-            if c == 0:
-                spread_chunk(3)
-                copy_tb(3)
             if c in (2, 4):
                 spread_chunk(c + 3)
                 copy_tb(c + 3)
             evict(c, 3, last)
-            if c == 0:
-                sums_quarter(2, 1)
             if c in (1, 3):
                 copy_tb(c + 3)
             if c == 2:

@@ -24,6 +24,7 @@ CH = 4096
 QUARTER = 1024
 CHUNK = 512
 NCHUNK = 8
+PAIRED = (1, 2, 3, 4, 5, 6, 7)
 TWO_ONES = 0x3F803F80
 HALF = 256
 W0 = QUARTER + 64
@@ -190,6 +191,7 @@ def tile_shiftconv_kernel(tc, x, w_pw, out):
         codes = {}
         scales = {}
         accs = {}
+        results = {}
 
         def direct(piece):
             first, n = span(piece)
@@ -330,12 +332,20 @@ def tile_shiftconv_kernel(tc, x, w_pw, out):
         def evict(piece, bank, on_vector):
             first, n = span(piece)
             per_bank = CHUNK // n
-            res = keep.tile([P, per_bank, n], F32, name="res%s_%d" % (piece, bank))
-            if on_vector:
-                nc.vector.tensor_copy(out=res[:], in_=accs[(piece, bank)][:])
+            if piece in PAIRED:
+                if bank % 2 == 0:
+                    results[piece] = keep.tile([P, 2, n], F32, name="res%s_%d" % (piece, bank))
+                res = results[piece][:, bank % 2 : bank % 2 + 1, :]
             else:
-                nc.scalar.copy(out=res[:], in_=accs[(piece, bank)][:])
-            nc.sync.dma_start(out=out_v[:, per_bank * bank : per_bank * (bank + 1), first : first + n], in_=res[:])
+                res = keep.tile([P, per_bank, n], F32, name="res%s_%d" % (piece, bank))[:]
+            if on_vector:
+                nc.vector.tensor_copy(out=res, in_=accs[(piece, bank)][:])
+            else:
+                nc.scalar.copy(out=res, in_=accs[(piece, bank)][:])
+            if piece not in PAIRED:
+                nc.sync.dma_start(out=out_v[:, per_bank * bank : per_bank * (bank + 1), first : first + n], in_=res)
+            elif bank % 2 == 1:
+                nc.sync.dma_start(out=out_v[:, bank - 1 : bank + 1, first : first + n], in_=results[piece][:])
 
         direct("a")
         round_direct("a")

@@ -24,7 +24,6 @@ CH = 4096
 QUARTER = 1024
 CHUNK = 512
 NCHUNK = 8
-PAIRED = (1, 2, 3, 4, 5, 6, 7)
 TWO_ONES = 0x3F803F80
 HALF = 256
 W0 = QUARTER + 64
@@ -293,7 +292,7 @@ def tile_shiftconv_kernel(tc, x, w_pw, out):
         def expand(piece):
             n = span(piece)[1]
             grouped = keep.tile([P, n, 4], BF16, name="grouped%s" % piece, align_bytes=64)
-            nc.vector.tensor_copy(out=grouped[:], in_=tbs[piece][:].unsqueeze(2).to_broadcast([P, n, 4]))
+            nc.vector.tensor_copy(out=grouped[:], in_=tbs[piece][:, 0:n].unsqueeze(2).to_broadcast([P, n, 4]))
             groupeds[piece] = grouped
 
         def quantise(piece):
@@ -332,20 +331,17 @@ def tile_shiftconv_kernel(tc, x, w_pw, out):
         def evict(piece, bank, on_vector):
             first, n = span(piece)
             per_bank = CHUNK // n
-            if piece in PAIRED:
-                if bank % 2 == 0:
-                    results[piece] = keep.tile([P, 2, n], F32, name="res%s_%d" % (piece, bank))
-                res = results[piece][:, bank % 2 : bank % 2 + 1, :]
-            else:
-                res = keep.tile([P, per_bank, n], F32, name="res%s_%d" % (piece, bank))[:]
+            if bank % 2 == 0:
+                results[piece] = keep.tile([P, 2 * per_bank, n], F32, name="res%s_%d" % (piece, bank))
+            res = results[piece][:, per_bank * (bank % 2) : per_bank * (bank % 2 + 1), :]
             if on_vector:
                 nc.vector.tensor_copy(out=res, in_=accs[(piece, bank)][:])
             else:
                 nc.scalar.copy(out=res, in_=accs[(piece, bank)][:])
-            if piece not in PAIRED:
-                nc.sync.dma_start(out=out_v[:, per_bank * bank : per_bank * (bank + 1), first : first + n], in_=res)
-            elif bank % 2 == 1:
-                nc.sync.dma_start(out=out_v[:, bank - 1 : bank + 1, first : first + n], in_=results[piece][:])
+            if bank % 2 == 1:
+                nc.sync.dma_start(
+                    out=out_v[:, per_bank * (bank - 1) : per_bank * (bank + 1), first : first + n], in_=results[piece][:]
+                )
 
         direct("a")
         round_direct("a")
@@ -410,9 +406,8 @@ def tile_shiftconv_kernel(tc, x, w_pw, out):
             evict(c, 2, False)
             if c in (2, 4):
                 spread_chunk(c + 3)
-                copy_tb(c + 3)
             evict(c, 3, last)
-            if c in (1, 3):
+            if c < 5:
                 copy_tb(c + 3)
             if c == 2:
                 sums_quarter(3, 1)

@@ -57,6 +57,9 @@ def tile_shiftconv_kernel(tc, x, w_pw, out):
         ps_mx = ctx.enter_context(tc.psum_pool(name="ps_mx", bufs=5))
         ctx.enter_context(tc.manual_schedule())
 
+        head = keep.tile([P, 3, 32], BF16, name="head")
+        nc.vector.memset(head[:, :, 0:8].bitcast(I32), 0)
+
         warm_in = keep.tile([P, 512], BF16, name="warm_in", align_bytes=64)
         warm_codes = keep.tile([P, P], U32, name="warm_codes", align_bytes=64)
         warm_scales = keep.tile([P, P], U8, name="warm_scales", align_bytes=64)
@@ -79,13 +82,9 @@ def tile_shiftconv_kernel(tc, x, w_pw, out):
 
         xt0 = keep.tile([P, 64 + 3 * W0], BF16, name="xt0")
         blocks = xt0[:, 64 : 64 + 3 * W0].rearrange("p (i m) -> p i m", i=3)
-        head = keep.tile([P, 3, 16], BF16, name="head")
         xq = keep.tile([P, 2, 3 * QUARTER], BF16, name="xq")
         x8 = keep.tile([P, QUARTER], BF16, name="x8")
         w_sb = keep.tile([P, 4, 512], BF16, name="w_sb")
-        nc.gpsimd.memset(head[:], 0.0)
-        nc.gpsimd.memset(xt0[:, 0:80], 0.0)
-        nc.gpsimd.memset(blocks[:, 1:3, 0:16], 0.0)
 
         def channel_rows(shift):
             return x_flat[shift : shift + 252 * CH].rearrange("(i r c) -> r i c", i=3, r=84)
@@ -93,8 +92,7 @@ def tile_shiftconv_kernel(tc, x, w_pw, out):
         def load_first_quarter(lo, hi):
             nc.sync.dma_start(out=blocks[1:P:2, :, lo:hi], in_=channel_rows(0)[20:84, :, lo:hi])
             nc.sync.dma_start(out=blocks[2:P:4, :, lo:hi], in_=channel_rows(1)[52:84, :, lo:hi])
-            first = max(lo, 16)
-            nc.sync.dma_start(out=blocks[0:P:4, :, first:hi], in_=channel_rows(15)[0:32, :, first - 16 : hi - 16])
+            nc.sync.dma_start(out=blocks[0:P:4, :, lo:hi], in_=channel_rows(15)[0:32, :, lo - 16 : hi - 16])
 
         def load_pair(e, lo, hi):
             g = PAIR_FIRST[e]
@@ -103,8 +101,10 @@ def tile_shiftconv_kernel(tc, x, w_pw, out):
             both = x_flat[b : b + 2 * apart].rearrange("(k z) -> k z", k=2)[:, 0 : 32 * CH]
             nc.sync.dma_start(out=xq[e:P:4, :, lo:hi], in_=both.rearrange("k (r c) -> r k c", c=CH)[:, :, lo:hi])
 
-        nc.sync.dma_start(out=head[0:P:4, :, :], in_=channel_rows(0)[0:32, :, 0:16])
-        load_first_quarter(0, HALF + 64)
+        load_first_quarter(16, HALF + 64)
+        nc.sync.dma_start(out=head[1:P:2, :, 0:18], in_=channel_rows(CH - 1)[19:83, :, 0:18])
+        nc.sync.dma_start(out=head[2:P:4, :, 0:18], in_=channel_rows(0)[52:84, :, 0:18])
+        nc.sync.dma_start(out=head[0:P:4, :, 2:18], in_=channel_rows(0)[0:32, :, 0:16])
         nc.sync.dma_start(out=w_sb[:], in_=w_pw.rearrange("(o t) c -> o t c", t=4))
         load_first_quarter(HALF + 64, CHUNK + 64)
         load_first_quarter(CHUNK + 64, W0)
@@ -119,6 +119,7 @@ def tile_shiftconv_kernel(tc, x, w_pw, out):
         make_identity(nc, ident_f[:])
         direct_w = keep.tile([P, 4 * P], BF16, name="direct_w")
         nc.gpsimd.memset(direct_w[:], 0.0)
+        nc.gpsimd.memset(xt0[:, 0:64], 0.0)
         cm = keep.tile([P, 64], F32, name="cm")
         nc.gpsimd.memset(cm[:], 1.0)
         ident_b = keep.tile([P, P], BF16, name="ident_b")
@@ -158,7 +159,7 @@ def tile_shiftconv_kernel(tc, x, w_pw, out):
         )
         nab = keep.tile([P, 2], F32, name="nab")
         nc.vector.tensor_scalar(out=nab[:], in0=ab[:], scalar1=0.0, scalar2=None, op0=EQ)
-        nc.vector.tensor_tensor(out=blocks[:, :, 1:16], in0=blocks[:, :, 1:16], in1=head[:, :, 0:15], op=ADD)
+        nc.vector.tensor_copy(out=blocks[:, :, 0:16], in_=head[:, :, 1:17])
 
         sel_k = keep.tile([P, 4], BF16, name="sel_k")
         nc.scalar.copy(out=sel_k[:], in_=selr[:, 0, :])
@@ -351,10 +352,10 @@ def tile_shiftconv_kernel(tc, x, w_pw, out):
         w_flip(1)
         w_copy(1)
         direct("b")
+        round_direct_on_scalar("b")
         w_quantise(0)
         quantise("a")
         w_quantise(1)
-        round_direct("b")
         w_flip(2)
         w_copy(2)
         w_flip(3)

@@ -118,8 +118,8 @@ def tile_shiftconv_kernel(tc, x, w_pw, out):
         ident_f = keep.tile([P, P], F32, name="ident_f")
         make_identity(nc, ident_f[:])
         direct_w = keep.tile([P, 4 * P], BF16, name="direct_w")
-        nc.gpsimd.memset(direct_w[:], 0.0)
-        nc.gpsimd.memset(xt0[:, 0:64], 0.0)
+        nc.vector.memset(direct_w[:], 0.0)
+        nc.vector.memset(xt0[:, 0:64], 0.0)
         cm = keep.tile([P, 64], F32, name="cm")
         nc.gpsimd.memset(cm[:], 1.0)
         ident_b = keep.tile([P, P], BF16, name="ident_b")

@@ -14,32 +14,22 @@ FP8X4 = mybir.dt.float8_e4m3fn_x4
 ADD = mybir.AluOpType.add
 MULT = mybir.AluOpType.mult
 EQ = mybir.AluOpType.is_equal
-COPY = mybir.ActivationFunctionType.Copy
 AX = mybir.AxisListType.X
 AXY = mybir.AxisListType.XY
 
 P = 128
-NG = 9
 CH = 4096
 QUARTER = 1024
 CHUNK = 512
-NCHUNK = 8
-TWO_ONES = 0x3F803F80
 HALF = 256
-W0 = QUARTER + 64
-PAIR_FIRST = (0, 1, 4, 5)
+TWO_ONES = 0x3F803F80
+PIECES = (("a", 1024, 256), ("b", 1280, 256), ("c", 1536, 256), ("d", 1792, 256), (4, 2048, 512), (5, 2560, 512), (6, 3072, 512), (7, 3584, 512), (0, 0, 512), (1, 512, 512))
+NCOL = 10
+RUN = 14
 
 
 def shift_of(g):
     return 64 * (g // 3 - 1) + (g % 3 - 1)
-
-
-def span(piece):
-    if piece == "a":
-        return 0, HALF
-    if piece == "b":
-        return HALF, HALF
-    return CHUNK * piece, CHUNK
 
 
 def first_channel(g):
@@ -56,9 +46,7 @@ def tile_shiftconv_kernel(tc, x, w_pw, out):
         ps_aux = ctx.enter_context(tc.psum_pool(name="ps_aux", bufs=2))
         ps_mx = ctx.enter_context(tc.psum_pool(name="ps_mx", bufs=5))
         ctx.enter_context(tc.manual_schedule())
-
-        head = keep.tile([P, 3, 32], BF16, name="head")
-        nc.vector.memset(head[:, :, 0:8].bitcast(I32), 0)
+        ctx.enter_context(nc.allow_low_precision(reason="sums of one nonzero term, exact in bfloat16"))
 
         warm_in = keep.tile([P, 512], BF16, name="warm_in", align_bytes=64)
         warm_codes = keep.tile([P, P], U32, name="warm_codes", align_bytes=64)
@@ -66,7 +54,7 @@ def tile_shiftconv_kernel(tc, x, w_pw, out):
         nc.vector.memset(warm_in[:].bitcast(I32), TWO_ONES)
         nc.vector.quantize_mx(out=warm_codes[:].bitcast(FP8X4), scales=warm_scales[:], in_=warm_in[:])
         idle = ps_mx.tile([P, 4, P], F32, tag="acc", name="idle")
-        for k in range(11):
+        for k in range(14):
             nc.tensor.matmul_mx(
                 out=idle[:, k % 4, :],
                 lhsT=warm_codes[:].bitcast(FP8X4),
@@ -80,158 +68,152 @@ def tile_shiftconv_kernel(tc, x, w_pw, out):
         x_flat = x.rearrange("b c h w -> (b c h w)")
         out_v = out.rearrange("b (o t) h w -> o (b t) (h w)", t=4)
 
-        xt0 = keep.tile([P, 64 + 3 * W0], BF16, name="xt0")
-        blocks = xt0[:, 64 : 64 + 3 * W0].rearrange("p (i m) -> p i m", i=3)
-        xq = keep.tile([P, 2, 3 * QUARTER], BF16, name="xq")
-        x8 = keep.tile([P, QUARTER], BF16, name="x8")
+        spans = {"a": (QUARTER, CHUNK), "b": (QUARTER + CHUNK, CHUNK), "c": (2 * QUARTER, QUARTER), "e": (3 * QUARTER, QUARTER), "d": (0, QUARTER)}
+        xs = {}
+        for name, (first, n) in spans.items():
+            xs[name] = keep.tile([P, 2, n], BF16, name="x_%s" % name)
+        x4a = keep.tile([P, CHUNK], BF16, name="x4a")
+        x4b = keep.tile([P, CHUNK], BF16, name="x4b")
         w_sb = keep.tile([P, 4, 512], BF16, name="w_sb")
+        fix_in = keep.tile([P, 16], BF16, name="fix_in")
+        fix = keep.tile([P, P], BF16, name="fix")
 
-        def channel_rows(shift):
-            return x_flat[shift : shift + 252 * CH].rearrange("(i r c) -> r i c", i=3, r=84)
-
-        def load_first_quarter(lo, hi):
-            nc.sync.dma_start(out=blocks[1:P:2, :, lo:hi], in_=channel_rows(0)[20:84, :, lo:hi])
-            nc.sync.dma_start(out=blocks[2:P:4, :, lo:hi], in_=channel_rows(1)[52:84, :, lo:hi])
-            nc.sync.dma_start(out=blocks[0:P:4, :, lo:hi], in_=channel_rows(15)[0:32, :, lo - 16 : hi - 16])
-
-        def load_pair(e, lo, hi):
-            g = PAIR_FIRST[e]
-            b = first_channel(g) * CH + QUARTER + shift_of(g)
-            apart = 56 * CH + shift_of(g + 2) - shift_of(g)
-            both = x_flat[b : b + 2 * apart].rearrange("(k z) -> k z", k=2)[:, 0 : 32 * CH]
-            nc.sync.dma_start(out=xq[e:P:4, :, lo:hi], in_=both.rearrange("k (r c) -> r k c", c=CH)[:, :, lo:hi])
-
-        load_first_quarter(16, HALF + 64)
-        nc.sync.dma_start(out=head[1:P:2, :, 0:18], in_=channel_rows(CH - 1)[19:83, :, 0:18])
-        nc.sync.dma_start(out=head[2:P:4, :, 0:18], in_=channel_rows(0)[52:84, :, 0:18])
-        nc.sync.dma_start(out=head[0:P:4, :, 2:18], in_=channel_rows(0)[0:32, :, 0:16])
-        nc.sync.dma_start(out=w_sb[:], in_=w_pw.rearrange("(o t) c -> o t c", t=4))
-        load_first_quarter(HALF + 64, CHUNK + 64)
-        load_first_quarter(CHUNK + 64, W0)
-        b8 = first_channel(8) * CH + shift_of(8)
-        nc.sync.dma_start(out=x8[:], in_=x_flat[b8 : b8 + P * QUARTER].rearrange("(r l) -> r l", l=QUARTER))
-        for e in range(4):
-            load_pair(e, 0, QUARTER)
-        for e in range(4):
-            load_pair(e, QUARTER, 3 * QUARTER)
-
-        ident_f = keep.tile([P, P], F32, name="ident_f")
-        make_identity(nc, ident_f[:])
-        direct_w = keep.tile([P, 4 * P], BF16, name="direct_w")
-        nc.vector.memset(direct_w[:], 0.0)
-        nc.vector.memset(xt0[:, 0:64], 0.0)
-        cm = keep.tile([P, 64], F32, name="cm")
-        nc.gpsimd.memset(cm[:], 1.0)
-        ident_b = keep.tile([P, P], BF16, name="ident_b")
-        make_identity(nc, ident_b[:])
-        mask = keep.tile([P, 3, 2, 36], F32, name="mask")
-        nc.gpsimd.memset(mask[:], 1.0)
-        s1 = {}
-        for q in range(1, 4):
-            s1[q] = keep.tile([P, 2, P], BF16, name="s1_%d" % q)
-            nc.gpsimd.memset(s1[q][:], 0.0)
-
-        selr = keep.tile([P, 2, 4], F32, name="selr")
-        nc.vector.tensor_reduce(
-            out=selr[:, 0, :], in_=ident_f[:, 0:112].rearrange("k (c e) -> k e c", e=4), axis=AX, op=ADD
-        )
-        nc.vector.tensor_reduce(
-            out=selr[:, 1, :], in_=ident_f[:, 16:128].rearrange("k (c e) -> k e c", e=4), axis=AX, op=ADD
-        )
-        sel_odd = keep.tile([P, 2], F32, name="sel_odd")
-        nc.vector.tensor_reduce(
-            out=sel_odd[:], in_=ident_f[:, 16:72].rearrange("k (c e) -> k e c", e=2), axis=AX, op=ADD
-        )
-        diagonal = direct_w[:, 0:510].rearrange("k (i z) -> k i z", z=170)
-        for j, rows_of_j in ((0, selr[:, 0, 0:1]), (1, sel_odd[:, 1:2]), (2, selr[:, 1, 2:3])):
-            nc.vector.tensor_copy(
-                out=diagonal[:, :, 14 * j : 14 * j + 14], in_=rows_of_j.unsqueeze(2).to_broadcast([P, 3, 14])
+        def load_pair(e, name):
+            first, n = spans[name]
+            b = first_channel(e) * CH + shift_of(e) + first
+            apart = (first_channel(e + 5) - first_channel(e)) * CH + shift_of(e + 5) - shift_of(e)
+            m = 2 if apart % 2 == 0 else 3
+            z = apart // m
+            assert z * m == apart
+            back = max(0, b + (m + 1) * z - 256 * CH)
+            both = x_flat[b - back : b - back + (m + 1) * z].rearrange("(k z) -> k z", z=z)
+            nc.sync.dma_start(
+                out=xs[name][e:P:4, :, :],
+                in_=both[0 : m + 1 : m, back : back + 32 * CH].rearrange("k (r c) -> r k c", c=CH)[:, :, 0:n],
             )
-        nc.vector.tensor_copy(out=direct_w[:, P + 126 : P + 128], in_=sel_odd[:, 1:2].to_broadcast([P, 2]))
-        cs = keep.tile([P, 3], F32, name="cs")
+
+        def load_one(g, name, skip):
+            first, n = spans[name]
+            b = first_channel(g) * CH + shift_of(g) + first + skip
+            nc.sync.dma_start(
+                out=xs[name][g % 5 : P : 4, g // 5, skip:n],
+                in_=x_flat[b : b + 32 * CH].rearrange("(r c) -> r c", c=CH)[:, 0 : n - skip],
+            )
+
+        x4_rows = x_flat[first_channel(4) * CH : first_channel(4) * CH + P * QUARTER].rearrange("(r l) -> r l", l=QUARTER)
+        for e in range(4):
+            load_pair(e, "a")
+        nc.sync.dma_start(out=x4a[:], in_=x4_rows[:, 0:CHUNK])
+        nc.sync.dma_start(out=w_sb[:], in_=w_pw.rearrange("(o t) c -> o t c", t=4))
+        for e in range(4):
+            load_pair(e, "b")
+        nc.sync.dma_start(out=x4b[:], in_=x4_rows[:, CHUNK:QUARTER])
+        for e in range(4):
+            load_pair(e, "c")
+        for e in range(4):
+            load_pair(e, "e")
+
+        ident = keep.tile([P, P], F32, name="ident")
+        make_identity(nc, ident[:])
+        nc.gpsimd.memset(xs["d"][:, 0, 0:80], 0.0)
+        nc.gpsimd.memset(fix_in[:], 0.0)
+        nc.gpsimd.memset(fix[:], 0.0)
+
+        for e in range(1, 4):
+            load_pair(e, "d")
+        load_one(5, "d", 0)
+        load_one(0, "d", 66)
+        nc.sync.dma_start(
+            out=fix_in[0:P:4, 0:2], in_=x_flat[0 : 32 * CH].rearrange("(r c) -> r c", c=CH)[:, 0:2]
+        )
+
+        direct_w = keep.tile([P, 512], BF16, name="direct_w")
+        nc.vector.memset(direct_w[:], 0.0)
+        sel = keep.tile([P, 2, 4], BF16, name="sel")
         nc.vector.tensor_reduce(
-            out=cs[:], in_=ident_f[:, 0:126].rearrange("p (i j r) -> p j i r", i=3, j=3), axis=AXY, op=ADD
+            out=sel[:],
+            in_=ident[:, 0:112].rearrange("p (c e) -> p e c", e=4).unsqueeze(1).to_broadcast([P, 2, 4, 28]),
+            axis=AX,
+            op=ADD,
         )
-        nc.vector.tensor_scalar(out=cm[:, 0:64:63], in0=cs[:, 0:3:2], scalar1=0.0, scalar2=None, op0=EQ)
-        ab = keep.tile([P, 2], F32, name="ab")
+        nc.vector.tensor_reduce(out=sel[:, 1, 3:4], in_=ident[:, 19:128:4], axis=AX, op=ADD)
+        runs = direct_w[:, 0:396].rearrange("p (k z) -> p k z", z=198)[:, :, 0:56].rearrange(
+            "p k (e s) -> p k e s", s=RUN
+        )
+        nc.vector.tensor_copy(out=runs, in_=sel[:].unsqueeze(3).to_broadcast([P, 2, 4, RUN]))
+        nc.vector.tensor_copy(out=direct_w[:, 256 + 56 : 256 + 70], in_=sel[:, 0, 1:2].to_broadcast([P, RUN]))
+        nc.vector.tensor_copy(out=direct_w[:, 256 + 126 : 256 + 128], in_=sel[:, 0, 1:2].to_broadcast([P, 2]))
+        edge = keep.tile([P, 4], BF16, name="edge")
         nc.vector.tensor_reduce(
-            out=ab[:], in_=ident_f[:].rearrange("p (h w) -> p w h", w=64)[:, 0:64:63, :], axis=AX, op=ADD
+            out=edge[:, 0:4:3],
+            in_=ident[:].rearrange("p (c e) -> p c e", e=4)[:, :, 1:3].unsqueeze(1).to_broadcast([P, 2, 32, 2]),
+            axis=AXY,
+            op=ADD,
         )
-        nab = keep.tile([P, 2], F32, name="nab")
-        nc.vector.tensor_scalar(out=nab[:], in0=ab[:], scalar1=0.0, scalar2=None, op0=EQ)
-        nc.vector.tensor_copy(out=blocks[:, :, 0:16], in_=head[:, :, 1:17])
+        nc.vector.tensor_scalar(out=edge[:, 1:3], in0=sel[:, 0, 1:3], scalar1=0.0, scalar2=None, op0=EQ)
+        edge_v = edge[:].rearrange("p (w k) -> p k w", k=2)
 
-        sel_k = keep.tile([P, 4], BF16, name="sel_k")
-        nc.scalar.copy(out=sel_k[:], in_=selr[:, 0, :])
-        sel_8 = keep.tile([P, 4], BF16, name="sel_8")
-        nc.scalar.copy(out=sel_8[:], in_=selr[:, 1, :])
-        mv = mask[:].rearrange("p a h (c i j) -> p (a h c i) j", i=3, j=3)
-        nc.scalar.copy(out=mv[:, :, 0:3:2], in_=nab[:].unsqueeze(1).to_broadcast([P, 72, 2]))
-        nc.gpsimd.memset(mask[64:128, 2, 1, 33:36], 0.0)
-        spread = keep.tile([P, 4, P], BF16, name="spread")
-        idg = ident_b[:, 0:36].rearrange("k (t g) -> k t g", g=NG)
-        nc.scalar.copy(
-            out=spread[:, :, 0:126].rearrange("k t (g r) -> k t g r", r=14),
-            in_=idg.unsqueeze(3).to_broadcast([P, 4, NG, 14]),
-        )
-        nc.scalar.copy(out=spread[:, :, 126:128], in_=idg[:, :, 4:5].to_broadcast([P, 4, 2]))
+        def mask_edges(engine, name):
+            rows = spans[name][1] // 64
+            v = xs[name][:].rearrange("p k (h w) -> p k h w", w=64)[:, :, :, 0:64:63]
+            engine.tensor_tensor(out=v, in0=v, in1=edge_v.unsqueeze(2).to_broadcast([P, 2, rows, 2]), op=MULT)
 
-
-        sums_flat = ps_sum.tile([P, 224], F32, name="sums")
-        sums = sums_flat[:, 0:216].rearrange("p (q h c) -> p q h c", q=3, h=2)
+        sums = ps_sum.tile([P, 30, NCOL], F32, name="sums")
+        pieces = {}
+        for name, first, n in PIECES:
+            for t, (lo, m) in spans.items():
+                if lo <= first < lo + m:
+                    pieces[name] = (first, n, t, first - lo)
+        used = [0]
+        rows = {}
         gw = keep.tile([P, 4, P, 2], F32, name="gw", align_bytes=64)
         w_codes = keep.tile([P, 512], U32, name="w_codes", align_bytes=64)
         w_scales = keep.tile([P, 512], U8, name="w_scales", align_bytes=64)
         wts = {}
-        stt = {}
-        pts = {}
-        tps = {}
-        tbs = {}
+        twins = {}
+        spreads = {}
+        pairs = {}
         groupeds = {}
         codes = {}
         scales = {}
         accs = {}
         results = {}
 
+        def x4_window(first, n):
+            col = first % QUARTER
+            return x4a[:, col : col + n] if col < CHUNK else x4b[:, col - CHUNK : col - CHUNK + n]
+
         def direct(piece):
-            first, n = span(piece)
-            tp = ps_aux.tile([P, CHUNK], F32, tag="aux", name="tpd%s" % piece)
-            for i in range(3):
-                lo = W0 * i + first + 64 * i
-                nc.tensor.matmul(
-                    tp[:, 0:n], lhsT=direct_w[:, P * i : P * (i + 1)], rhs=xt0[:, lo : lo + n], start=i == 0, stop=i == 2
-                )
-            tps[piece] = tp
-
-        def round_direct(piece):
-            n = span(piece)[1]
-            tb = keep.tile([P, n], BF16, name="tb%s" % piece)
-            nc.vector.tensor_tensor(
-                out=tb[:].rearrange("p (h w) -> p h w", w=64),
-                in0=tps[piece][:, 0:n].rearrange("p (h w) -> p h w", w=64),
-                in1=cm[:].unsqueeze(1).to_broadcast([P, n // 64, 64]),
-                op=MULT,
-            )
-            tbs[piece] = tb
-
-        def round_direct_on_scalar(piece):
-            n = span(piece)[1]
-            tb = keep.tile([P, n], BF16, name="tb%s" % piece)
-            nc.scalar.copy(out=tb[:], in_=tps[piece][:, 0:n])
-            tbv = tb[:].rearrange("p (h w) -> p h w", w=64)
-            for col in (0, 63):
-                nc.scalar.activation(out=tbv[:, :, col], in_=tbv[:, :, col], func=COPY, scale=cm[:, col : col + 1])
-            tbs[piece] = tb
+            first, n, t, lo = pieces[piece]
+            dp = ps_aux.tile([P, 2 * n], BF16, tag="aux", name="dp%s" % piece)
+            for h in range(n // HALF):
+                for i in range(3):
+                    if i < 2:
+                        window = xs[t][:, i, lo + HALF * h : lo + HALF * (h + 1)]
+                    else:
+                        window = x4_window(first + HALF * h, HALF)
+                    nc.tensor.matmul(
+                        dp[:, CHUNK * h : CHUNK * (h + 1)].rearrange("p (n j) -> p n j", j=2),
+                        lhsT=direct_w[:, P * i : P * (i + 1)],
+                        rhs=window.unsqueeze(2).to_broadcast([P, HALF, 2]),
+                        start=i == 0,
+                        stop=i == 2,
+                    )
+            pairs[piece] = dp[:].bitcast(F32)
 
         def w_flip(t):
             wt = ps_mx.tile([P, 2, P], F32, tag="acc", name="wt%d" % t)
             words = w_sb[:, t, :].bitcast(F32).rearrange("o (p u) -> o u p", u=2)
             for u in range(2):
-                nc.tensor.transpose(wt[:, u, :], words[:, u, :], ident_f[:])
+                nc.tensor.transpose(wt[:, u, :], words[:, u, :], ident[:])
             wts[t] = wt
 
-        def w_copy(t):
-            nc.scalar.copy(out=gw[:, t, :, :], in_=wts[t][:].rearrange("p u o -> p o u"))
+        def w_copy(t, on_vector):
+            src = wts[t][:].rearrange("p u o -> p o u")
+            if on_vector:
+                nc.vector.tensor_copy(out=gw[:, t, :, :], in_=src)
+            else:
+                nc.scalar.copy(out=gw[:, t, :, :], in_=src)
 
         def w_quantise(t):
             cols = slice(P * t, P * (t + 1))
@@ -241,75 +223,68 @@ def tile_shiftconv_kernel(tc, x, w_pw, out):
                 in_=gw[:, t, :, :].rearrange("p o u -> p (o u)").bitcast(BF16),
             )
 
-        def sums_group8():
-            for ct in range(8):
+        def sum_piece(piece):
+            first, n, t, lo = pieces[piece]
+            q = first // QUARTER
+            base = used[0]
+            used[0] += n // P
+            rows[piece] = sums[:, base : base + n // P, :].rearrange("p t g -> p (t g)")
+            for k in range(n // P):
+                row = sums[:, base + k, :]
+                top = first + k == 0
+                at = lo + P * k
+                nc.tensor.matmul(row[:, 0:4], lhsT=xs[t][:, 0, at : at + P], rhs=sel[:, 0, :], start=True, stop=not top)
+                if top:
+                    nc.tensor.matmul(row[:, 0:4], lhsT=fix[:], rhs=sel[:, 0, :], start=False, stop=True)
+                nc.tensor.matmul(row[:, 5:9], lhsT=xs[t][:, 1, at : at + P], rhs=sel[:, 1, :], start=True, stop=True)
                 nc.tensor.matmul(
-                    sums[:, :, ct // 4, 9 * (ct % 4) + 8],
-                    lhsT=x8[:, P * ct : P * (ct + 1)],
-                    rhs=sel_8[:, 1:4],
+                    row[:, 4:10:5],
+                    lhsT=x4_window(first + P * k, P),
+                    rhs=sel[:, 0, q : q + 1].to_broadcast([P, 2]),
                     start=True,
                     stop=True,
                 )
 
-        def sums_quarter(q, k):
-            for ct in range(8):
-                col = 72 * (q - 1) + 36 * (ct // 4) + 9 * (ct % 4) + 2 * k
-                first = QUARTER * (q - 1) + P * ct
-                nc.tensor.matmul(
-                    sums_flat[:, col : col + 8].rearrange("p (a b) -> p a b", b=4)[:, :, 0:2],
-                    lhsT=xq[:, k, first : first + P],
-                    rhs=sel_k[:].rearrange("p (a b) -> p a b", b=2),
-                    start=True,
-                    stop=True,
-                )
+        def round_piece(piece):
+            n = NCOL * pieces[piece][1] // P
+            twin = keep.tile([P, n, 2], BF16, name="twin%s" % piece)
+            nc.vector.tensor_copy(out=twin[:], in_=rows[piece].unsqueeze(2).to_broadcast([P, n, 2]))
+            twins[piece] = twin
 
-        def round_sums(q):
-            nc.vector.tensor_tensor(out=s1[q][:, :, 0:36], in0=sums[:, q - 1], in1=mask[:, q - 1], op=MULT)
+        def spread_piece(piece):
+            n = NCOL * pieces[piece][1] // P
+            wide = keep.tile([P, n, RUN], F32, name="wide%s" % piece)
+            src = twins[piece][:].rearrange("p g j -> p (g j)").bitcast(F32)
+            nc.vector.tensor_copy(out=wide[:], in_=src.unsqueeze(2).to_broadcast([P, n, RUN]))
+            spreads[piece] = wide[:].rearrange("p g s -> p (g s)")
 
-        def flip_sums(q):
-            pt = ps_aux.tile([P, 2, P], BF16, tag="aux", name="pt%d" % q)
-            for h in range(2):
-                nc.tensor.transpose(pt[:, h, :], s1[q][:, h, :], ident_b[:])
-            pts[q] = pt
-
-        def keep_flipped(q):
-            t = keep.tile([P, 2, P], BF16, name="stt%d" % q)
-            nc.scalar.copy(out=t[:], in_=pts[q][:])
-            stt[q] = t
-
-        def spread_chunk(c):
-            tp = ps_aux.tile([P, 4, P], BF16, tag="aux", name="tp%d" % c)
-            for tl in range(4):
-                nc.tensor.matmul(
-                    tp[:, tl, :], lhsT=spread[:, tl, :], rhs=stt[c // 2][:, c % 2, :], start=True, stop=True
-                )
-            tps[c] = tp
-
-        def copy_tb(c):
-            tb = keep.tile([P, CHUNK], BF16, name="tb%d" % c)
-            nc.scalar.copy(out=tb[:], in_=tps[c][:].rearrange("p t n -> p (t n)"))
-            tbs[c] = tb
+        def flip_piece(piece):
+            n = pieces[piece][1] // P
+            pt = ps_aux.tile([P, n, P], F32, tag="aux", name="pt%s" % piece)
+            for k in range(n):
+                first = NCOL * RUN * k
+                nc.tensor.transpose(pt[:, k, :], spreads[piece][:, first : first + P], ident[:])
+            pairs[piece] = pt[:].rearrange("p t n -> p (t n)")
 
         def expand(piece):
-            n = span(piece)[1]
-            grouped = keep.tile([P, n, 4], BF16, name="grouped%s" % piece, align_bytes=64)
-            nc.vector.tensor_copy(out=grouped[:], in_=tbs[piece][:, 0:n].unsqueeze(2).to_broadcast([P, n, 4]))
+            n = pieces[piece][1]
+            grouped = keep.tile([P, 4 * n], BF16, name="grouped%s" % piece, align_bytes=64)
+            nc.scalar.copy(
+                out=grouped[:].bitcast(F32).rearrange("p (n j) -> p n j", j=2),
+                in_=pairs[piece].unsqueeze(2).to_broadcast([P, n, 2]),
+            )
             groupeds[piece] = grouped
 
         def quantise(piece):
-            n = span(piece)[1]
+            n = pieces[piece][1]
             cd = keep.tile([P, n], U32, name="codes%s" % piece, align_bytes=64)
             sc = keep.tile([P, n], U8, name="scales%s" % piece, align_bytes=64)
-            nc.vector.quantize_mx(
-                out=cd[:].bitcast(FP8X4),
-                scales=sc[:],
-                in_=groupeds[piece][:].rearrange("p n j -> p (n j)"),
-            )
+            nc.vector.quantize_mx(out=cd[:].bitcast(FP8X4), scales=sc[:], in_=groupeds[piece][:])
             codes[piece] = cd
             scales[piece] = sc
 
         def multiply_bank(piece, bank):
-            n = span(piece)[1]
+            n = pieces[piece][1]
             per_bank = CHUNK // n
             acc = ps_mx.tile([P, per_bank, n], F32, tag="acc", name="acc%s_%d" % (piece, bank))
             accs[(piece, bank)] = acc
@@ -325,92 +300,109 @@ def tile_shiftconv_kernel(tc, x, w_pw, out):
                     stop=True,
                 )
 
-        def multiply(piece):
-            for bank in range(4 * span(piece)[1] // CHUNK):
-                multiply_bank(piece, bank)
-
         def evict(piece, bank, on_vector):
-            first, n = span(piece)
+            first, n, _, _ = pieces[piece]
             per_bank = CHUNK // n
-            if bank % 2 == 0:
-                results[piece] = keep.tile([P, 2 * per_bank, n], F32, name="res%s_%d" % (piece, bank))
-            res = results[piece][:, per_bank * (bank % 2) : per_bank * (bank % 2 + 1), :]
+            whole = 2 if n == CHUNK else 1
+            if bank % whole == 0:
+                results[piece] = keep.tile([P, whole * per_bank, n], F32, name="res%s_%d" % (piece, bank))
+            at = per_bank * (bank % whole)
+            dst = results[piece][:, at : at + per_bank, :]
             if on_vector:
-                nc.vector.tensor_copy(out=res, in_=accs[(piece, bank)][:])
+                nc.vector.tensor_copy(out=dst, in_=accs[(piece, bank)][:])
             else:
-                nc.scalar.copy(out=res, in_=accs[(piece, bank)][:])
-            if bank % 2 == 1:
+                nc.scalar.copy(out=dst, in_=accs[(piece, bank)][:])
+            if bank % whole == whole - 1:
+                lo = per_bank * (bank + 1 - whole)
                 nc.sync.dma_start(
-                    out=out_v[:, per_bank * (bank - 1) : per_bank * (bank + 1), first : first + n], in_=results[piece][:]
+                    out=out_v[:, lo : lo + whole * per_bank, first : first + n], in_=results[piece][:]
                 )
 
+        def mask_c():
+            mask_edges(nc.gpsimd, "c")
+            mask_edges(nc.gpsimd, "e")
+            bottom = xs["e"][:, 1, QUARTER - 64 : QUARTER]
+            nc.gpsimd.tensor_tensor(out=bottom, in0=bottom, in1=sel[:, 1, 0:1].to_broadcast([P, 64]), op=MULT)
+
+        def mask_d():
+            mask_edges(nc.gpsimd, "d")
+            top = xs["d"][:, 0, 0:64]
+            nc.gpsimd.tensor_tensor(out=top, in0=top, in1=sel[:, 0, 3:4].to_broadcast([P, 64]), op=MULT)
+            nc.gpsimd.tensor_copy(out=fix[:, 65:66], in_=fix_in[:, 0:1])
+
+        mask_c()
+        mask_d()
+        mask_edges(nc.vector, "a")
         direct("a")
-        round_direct("a")
         w_flip(0)
-        w_copy(0)
-        expand("a")
         w_flip(1)
-        w_copy(1)
-        direct("b")
-        round_direct_on_scalar("b")
-        w_quantise(0)
-        quantise("a")
-        w_quantise(1)
+        expand("a")
+        w_copy(0, True)
+        w_copy(1, False)
         w_flip(2)
-        w_copy(2)
         w_flip(3)
-        w_copy(3)
-        direct(1)
-        round_direct_on_scalar(1)
+        direct("b")
+        quantise("a")
+        w_quantise(0)
+        w_copy(2, False)
+        w_quantise(1)
+        w_copy(3, True)
         multiply_bank("a", 0)
         expand("b")
-        sums_group8()
-        sums_quarter(1, 0)
-        sums_quarter(1, 1)
         w_quantise(2)
         w_quantise(3)
-        evict("a", 0, False)
+        mask_edges(nc.vector, "b")
         multiply_bank("a", 1)
+        evict("a", 0, False)
+        direct("c")
         quantise("b")
-        round_sums(1)
-        flip_sums(1)
-        keep_flipped(1)
-        evict("a", 1, False)
-        multiply("b")
-        expand(1)
-        spread_chunk(2)
-        copy_tb(2)
-        evict("b", 0, False)
-        sums_quarter(2, 0)
-        quantise(1)
-        spread_chunk(3)
+        evict("a", 1, True)
+        multiply_bank("b", 0)
+        expand("c")
+        multiply_bank("b", 1)
+        evict("b", 0, True)
+        direct("d")
+        quantise("c")
+        sum_piece(4)
         evict("b", 1, False)
-        copy_tb(3)
-        sums_quarter(2, 1)
-
-        for c in range(1, NCHUNK):
-            last = c == NCHUNK - 1
-            helps = c in (2, 4, 5, 6, 7)
-            multiply(c)
-            evict(c, 0, False)
-            if not last:
-                expand(c + 1)
-            evict(c, 1, helps)
-            if c in (1, 3):
-                q = (c + 3) // 2
-                round_sums(q)
-                flip_sums(q)
-                keep_flipped(q)
-                if c == 1:
-                    sums_quarter(3, 0)
-                spread_chunk(2 * q)
+        multiply_bank("c", 0)
+        multiply_bank("c", 1)
+        expand("d")
+        round_piece(4)
+        spread_piece(4)
+        evict("c", 0, True)
+        quantise("d")
+        sum_piece(5)
+        evict("c", 1, False)
+        flip_piece(4)
+        multiply_bank("d", 0)
+        multiply_bank("d", 1)
+        expand(4)
+        round_piece(5)
+        spread_piece(5)
+        evict("d", 0, True)
+        sum_piece(6)
+        evict("d", 1, False)
+        quantise(4)
+        flip_piece(5)
+        round_piece(6)
+        spread_piece(6)
+        order = (4, 5, 6, 7, 0, 1)
+        for i, c in enumerate(order):
+            for bank in range(4):
+                multiply_bank(c, bank)
+            if i + 1 < 6:
+                expand(order[i + 1])
+            if i + 2 < 6:
+                flip_piece(order[i + 2])
+            if i + 3 < 6:
+                sum_piece(order[i + 3])
+            evict(c, 0, True)
+            evict(c, 1, False)
+            if i + 1 < 6:
+                quantise(order[i + 1])
             evict(c, 2, False)
-            if c in (2, 4):
-                spread_chunk(c + 3)
-            evict(c, 3, last)
-            if c < 5:
-                copy_tb(c + 3)
-            if c == 2:
-                sums_quarter(3, 1)
-            if not last:
-                quantise(c + 1)
+            evict(c, 3, True)
+            if i + 3 < 6:
+                round_piece(order[i + 3])
+                spread_piece(order[i + 3])

@@ -23,7 +23,7 @@ QUARTER = 1024
 CHUNK = 512
 HALF = 256
 TWO_ONES = 0x3F803F80
-PIECES = (("a", 1024, 256), ("b", 1280, 256), ("c", 1536, 256), ("d", 1792, 256), (4, 2048, 512), (5, 2560, 512), (6, 3072, 512), (7, 3584, 512), (0, 0, 512), (1, 512, 512))
+PIECES = (("a", 1024, 256), ("b", 1280, 256), (3, 1536, 512), (4, 2048, 512), (5, 2560, 512), (6, 3072, 512), (7, 3584, 512), (0, 0, 512), (1, 512, 512))
 NCOL = 10
 RUN = 14
 
@@ -42,9 +42,9 @@ def tile_shiftconv_kernel(tc, x, w_pw, out):
     nc = tc.nc
     with ExitStack() as ctx:
         keep = ctx.enter_context(tc.tile_pool(name="keep", bufs=1))
-        ps_sum = ctx.enter_context(tc.psum_pool(name="ps_sum", bufs=1))
+        ps_sum = ctx.enter_context(tc.psum_pool(name="ps_sum", bufs=2))
         ps_aux = ctx.enter_context(tc.psum_pool(name="ps_aux", bufs=2))
-        ps_mx = ctx.enter_context(tc.psum_pool(name="ps_mx", bufs=5))
+        ps_mx = ctx.enter_context(tc.psum_pool(name="ps_mx", bufs=4))
         ctx.enter_context(tc.manual_schedule())
         ctx.enter_context(nc.allow_low_precision(reason="sums of one nonzero term, exact in bfloat16"))
 
@@ -158,7 +158,6 @@ def tile_shiftconv_kernel(tc, x, w_pw, out):
             v = xs[name][:].rearrange("p k (h w) -> p k h w", w=64)[:, :, :, 0:64:63]
             engine.tensor_tensor(out=v, in0=v, in1=edge_v.unsqueeze(2).to_broadcast([P, 2, rows, 2]), op=MULT)
 
-        sums = ps_sum.tile([P, 30, NCOL], F32, name="sums")
         pieces = {}
         for name, first, n in PIECES:
             for t, (lo, m) in spans.items():
@@ -226,11 +225,10 @@ def tile_shiftconv_kernel(tc, x, w_pw, out):
         def sum_piece(piece):
             first, n, t, lo = pieces[piece]
             q = first // QUARTER
-            base = used[0]
-            used[0] += n // P
-            rows[piece] = sums[:, base : base + n // P, :].rearrange("p t g -> p (t g)")
+            sums = ps_sum.tile([P, n // P, NCOL], F32, tag="sums", name="sums%s" % piece)
+            rows[piece] = sums[:].rearrange("p t g -> p (t g)")
             for k in range(n // P):
-                row = sums[:, base + k, :]
+                row = sums[:, k, :]
                 top = first + k == 0
                 at = lo + P * k
                 nc.tensor.matmul(row[:, 0:4], lhsT=xs[t][:, 0, at : at + P], rhs=sel[:, 0, :], start=True, stop=not top)
@@ -330,6 +328,7 @@ def tile_shiftconv_kernel(tc, x, w_pw, out):
             nc.gpsimd.tensor_tensor(out=top, in0=top, in1=sel[:, 0, 3:4].to_broadcast([P, 64]), op=MULT)
             nc.gpsimd.tensor_copy(out=fix[:, 65:66], in_=fix_in[:, 0:1])
 
+        mask_edges(nc.gpsimd, "b")
         mask_c()
         mask_d()
         mask_edges(nc.vector, "a")
@@ -347,62 +346,38 @@ def tile_shiftconv_kernel(tc, x, w_pw, out):
         w_copy(2, False)
         w_quantise(1)
         w_copy(3, True)
-        multiply_bank("a", 0)
-        expand("b")
-        w_quantise(2)
-        w_quantise(3)
-        mask_edges(nc.vector, "b")
-        multiply_bank("a", 1)
-        evict("a", 0, False)
-        direct("c")
-        quantise("b")
-        evict("a", 1, True)
-        multiply_bank("b", 0)
-        expand("c")
-        multiply_bank("b", 1)
-        evict("b", 0, True)
-        direct("d")
-        quantise("c")
-        sum_piece(4)
-        evict("b", 1, False)
-        multiply_bank("c", 0)
-        multiply_bank("c", 1)
-        expand("d")
-        round_piece(4)
-        spread_piece(4)
-        evict("c", 0, True)
-        quantise("d")
-        sum_piece(5)
-        evict("c", 1, False)
-        flip_piece(4)
-        multiply_bank("d", 0)
-        multiply_bank("d", 1)
-        expand(4)
-        round_piece(5)
-        spread_piece(5)
-        evict("d", 0, True)
-        sum_piece(6)
-        evict("d", 1, False)
-        quantise(4)
-        flip_piece(5)
-        round_piece(6)
-        spread_piece(6)
-        order = (4, 5, 6, 7, 0, 1)
-        for i, c in enumerate(order):
-            for bank in range(4):
-                multiply_bank(c, bank)
-            if i + 1 < 6:
-                expand(order[i + 1])
-            if i + 2 < 6:
-                flip_piece(order[i + 2])
-            if i + 3 < 6:
-                sum_piece(order[i + 3])
-            evict(c, 0, True)
-            evict(c, 1, False)
-            if i + 1 < 6:
-                quantise(order[i + 1])
-            evict(c, 2, False)
-            evict(c, 3, True)
-            if i + 3 < 6:
-                round_piece(order[i + 3])
-                spread_piece(order[i + 3])
+        sum_piece(3)
+        seq = ("a", "b", 3, 4, 5, 6, 7, 0, 1)
+        for i, p in enumerate(seq):
+            banks = 4 * pieces[p][1] // CHUNK
+            nxt = seq[i + 1] if i + 1 < len(seq) else None
+            sec = seq[i + 2] if i + 2 < len(seq) else None
+            thd = seq[i + 3] if i + 3 < len(seq) else None
+            multiply_bank(p, 0)
+            if nxt is not None:
+                expand(nxt)
+            if i == 0:
+                w_quantise(2)
+                w_quantise(3)
+                round_piece(3)
+            for bank in range(1, banks):
+                multiply_bank(p, bank)
+            if i == 0:
+                spread_piece(3)
+            if sec is not None:
+                flip_piece(sec)
+            for j in (range(i + 3, i + 5) if i == 1 else range(i + 3 + min(i, 1), i + 4 + min(i, 1))):
+                if j < len(seq):
+                    sum_piece(seq[j])
+            evict(p, 0, True)
+            evict(p, 1, False)
+            if nxt is not None:
+                quantise(nxt)
+            if banks == 4:
+                evict(p, 2, False)
+            if thd is not None:
+                round_piece(thd)
+            if banks == 4:
+                evict(p, 3, True)
+            if thd is not None:
+                spread_piece(thd)

@@ -87,7 +87,7 @@ def tile_shiftconv_kernel(tc, x, w_pw, out):
             assert z * m == apart
             back = max(0, b + (m + 1) * z - 256 * CH)
             both = x_flat[b - back : b - back + (m + 1) * z].rearrange("(k z) -> k z", z=z)
-            nc.sync.dma_start(
+            (nc.scalar if name == "a" and e % 2 == 1 else nc.sync).dma_start(
                 out=xs[name][e:P:4, :, :],
                 in_=both[0 : m + 1 : m, back : back + 32 * CH].rearrange("k (r c) -> r k c", c=CH)[:, :, 0:n],
             )
@@ -104,7 +104,7 @@ def tile_shiftconv_kernel(tc, x, w_pw, out):
         for e in range(4):
             load_pair(e, "a")
         nc.sync.dma_start(out=x4a[:], in_=x4_rows[:, 0:CHUNK])
-        nc.sync.dma_start(out=w_sb[:], in_=w_pw.rearrange("(o t) c -> o t c", t=4))
+        nc.scalar.dma_start(out=w_sb[:], in_=w_pw.rearrange("(o t) c -> o t c", t=4))
         for e in range(4):
             load_pair(e, "b")
         nc.sync.dma_start(out=x4b[:], in_=x4_rows[:, CHUNK:QUARTER])
@@ -152,6 +152,21 @@ def tile_shiftconv_kernel(tc, x, w_pw, out):
         )
         nc.vector.tensor_scalar(out=edge[:, 1:3], in0=sel[:, 0, 1:3], scalar1=0.0, scalar2=None, op0=EQ)
         edge_v = edge[:].rearrange("p (w k) -> p k w", k=2)
+
+        ends = keep.tile([P, 2], F32, name="ends")
+        kept = keep.tile([P, NCOL], F32, name="kept")
+
+        nc.gpsimd.memset(kept[:], 1.0)
+
+        def make_kept():
+            nc.vector.tensor_reduce(
+                out=ends[:], in_=ident[:].rearrange("p (h w) -> p w h", w=64)[:, 0:64:63, :], axis=AX, op=ADD
+            )
+            nc.vector.tensor_scalar(out=ends[:], in0=ends[:], scalar1=0.0, scalar2=None, op0=EQ)
+            nc.vector.tensor_copy(
+                out=kept[:, 0:9].rearrange("p (i j) -> p i j", j=3)[:, :, 0:3:2],
+                in_=ends[:].unsqueeze(1).to_broadcast([P, 3, 2]),
+            )
 
         def mask_edges(engine, name):
             rows = spans[name][1] // 64
@@ -246,7 +261,13 @@ def tile_shiftconv_kernel(tc, x, w_pw, out):
         def round_piece(piece):
             n = NCOL * pieces[piece][1] // P
             twin = keep.tile([P, n, 2], BF16, name="twin%s" % piece)
-            nc.vector.tensor_copy(out=twin[:], in_=rows[piece].unsqueeze(2).to_broadcast([P, n, 2]))
+            m = n // NCOL
+            nc.vector.tensor_tensor(
+                out=twin[:].rearrange("p (t g) j -> p t g j", g=NCOL),
+                in0=rows[piece].rearrange("p (t g) -> p t g", g=NCOL).unsqueeze(3).to_broadcast([P, m, NCOL, 2]),
+                in1=kept[:].unsqueeze(1).unsqueeze(3).to_broadcast([P, m, NCOL, 2]),
+                op=MULT,
+            )
             twins[piece] = twin
 
         def spread_piece(piece):
@@ -317,21 +338,18 @@ def tile_shiftconv_kernel(tc, x, w_pw, out):
                 )
 
         def mask_c():
-            mask_edges(nc.gpsimd, "c")
-            mask_edges(nc.gpsimd, "e")
             bottom = xs["e"][:, 1, QUARTER - 64 : QUARTER]
             nc.gpsimd.tensor_tensor(out=bottom, in0=bottom, in1=sel[:, 1, 0:1].to_broadcast([P, 64]), op=MULT)
 
         def mask_d():
-            mask_edges(nc.gpsimd, "d")
             top = xs["d"][:, 0, 0:64]
             nc.gpsimd.tensor_tensor(out=top, in0=top, in1=sel[:, 0, 3:4].to_broadcast([P, 64]), op=MULT)
             nc.gpsimd.tensor_copy(out=fix[:, 65:66], in_=fix_in[:, 0:1])
 
-        mask_edges(nc.gpsimd, "b")
         mask_c()
         mask_d()
         mask_edges(nc.vector, "a")
+        make_kept()
         direct("a")
         w_flip(0)
         w_flip(1)

@@ -52,9 +52,11 @@ def tile_shiftconv_kernel(tc, x, w_pw, out):
         warm_codes = keep.tile([P, P], U32, name="warm_codes", align_bytes=64)
         warm_scales = keep.tile([P, P], U8, name="warm_scales", align_bytes=64)
         nc.vector.memset(warm_in[:].bitcast(I32), TWO_ONES)
+        direct_w = keep.tile([P, 512], BF16, name="direct_w")
+        nc.vector.memset(direct_w[:], 0.0)
         nc.vector.quantize_mx(out=warm_codes[:].bitcast(FP8X4), scales=warm_scales[:], in_=warm_in[:])
         idle = ps_mx.tile([P, 4, P], F32, tag="acc", name="idle")
-        for k in range(14):
+        for k in range(20):
             nc.tensor.matmul_mx(
                 out=idle[:, k % 4, :],
                 lhsT=warm_codes[:].bitcast(FP8X4),
@@ -68,7 +70,7 @@ def tile_shiftconv_kernel(tc, x, w_pw, out):
         x_flat = x.rearrange("b c h w -> (b c h w)")
         out_v = out.rearrange("b (o t) h w -> o (b t) (h w)", t=4)
 
-        spans = {"a": (QUARTER, CHUNK), "b": (QUARTER + CHUNK, CHUNK), "c": (2 * QUARTER, QUARTER), "e": (3 * QUARTER, QUARTER), "d": (0, QUARTER)}
+        spans = {"a": (QUARTER, CHUNK), "b": (QUARTER + CHUNK, CHUNK), "c": (2 * QUARTER, 2 * QUARTER), "d": (0, QUARTER)}
         xs = {}
         for name, (first, n) in spans.items():
             xs[name] = keep.tile([P, 2, n], BF16, name="x_%s" % name)
@@ -110,8 +112,6 @@ def tile_shiftconv_kernel(tc, x, w_pw, out):
         nc.sync.dma_start(out=x4b[:], in_=x4_rows[:, CHUNK:QUARTER])
         for e in range(4):
             load_pair(e, "c")
-        for e in range(4):
-            load_pair(e, "e")
 
         ident = keep.tile([P, P], F32, name="ident")
         make_identity(nc, ident[:])
@@ -127,30 +127,28 @@ def tile_shiftconv_kernel(tc, x, w_pw, out):
             out=fix_in[0:P:4, 0:2], in_=x_flat[0 : 32 * CH].rearrange("(r c) -> r c", c=CH)[:, 0:2]
         )
 
-        direct_w = keep.tile([P, 512], BF16, name="direct_w")
-        nc.vector.memset(direct_w[:], 0.0)
         sel = keep.tile([P, 2, 4], BF16, name="sel")
+        edge = keep.tile([P, 4], BF16, name="edge")
         nc.vector.tensor_reduce(
             out=sel[:],
             in_=ident[:, 0:112].rearrange("p (c e) -> p e c", e=4).unsqueeze(1).to_broadcast([P, 2, 4, 28]),
             axis=AX,
             op=ADD,
         )
-        nc.vector.tensor_reduce(out=sel[:, 1, 3:4], in_=ident[:, 19:128:4], axis=AX, op=ADD)
-        runs = direct_w[:, 0:396].rearrange("p (k z) -> p k z", z=198)[:, :, 0:56].rearrange(
-            "p k (e s) -> p k e s", s=RUN
-        )
-        nc.vector.tensor_copy(out=runs, in_=sel[:].unsqueeze(3).to_broadcast([P, 2, 4, RUN]))
-        nc.vector.tensor_copy(out=direct_w[:, 256 + 56 : 256 + 70], in_=sel[:, 0, 1:2].to_broadcast([P, RUN]))
-        nc.vector.tensor_copy(out=direct_w[:, 256 + 126 : 256 + 128], in_=sel[:, 0, 1:2].to_broadcast([P, 2]))
-        edge = keep.tile([P, 4], BF16, name="edge")
         nc.vector.tensor_reduce(
             out=edge[:, 0:4:3],
             in_=ident[:].rearrange("p (c e) -> p c e", e=4)[:, :, 1:3].unsqueeze(1).to_broadcast([P, 2, 32, 2]),
             axis=AXY,
             op=ADD,
         )
+        nc.vector.tensor_reduce(out=sel[:, 1, 3:4], in_=ident[:, 19:128:4], axis=AX, op=ADD)
         nc.vector.tensor_scalar(out=edge[:, 1:3], in0=sel[:, 0, 1:3], scalar1=0.0, scalar2=None, op0=EQ)
+        runs = direct_w[:, 0:396].rearrange("p (k z) -> p k z", z=198)[:, :, 0:56].rearrange(
+            "p k (e s) -> p k e s", s=RUN
+        )
+        nc.vector.tensor_copy(out=runs, in_=sel[:].unsqueeze(3).to_broadcast([P, 2, 4, RUN]))
+        nc.vector.tensor_copy(out=direct_w[:, 256 + 56 : 256 + 70], in_=sel[:, 0, 1:2].to_broadcast([P, RUN]))
+        nc.vector.tensor_copy(out=direct_w[:, 256 + 126 : 256 + 128], in_=sel[:, 0, 1:2].to_broadcast([P, 2]))
         edge_v = edge[:].rearrange("p (w k) -> p k w", k=2)
 
         ends = keep.tile([P, 2], F32, name="ends")
@@ -338,7 +336,7 @@ def tile_shiftconv_kernel(tc, x, w_pw, out):
                 )
 
         def mask_c():
-            bottom = xs["e"][:, 1, QUARTER - 64 : QUARTER]
+            bottom = xs["c"][:, 1, 2 * QUARTER - 64 : 2 * QUARTER]
             nc.gpsimd.tensor_tensor(out=bottom, in0=bottom, in1=sel[:, 1, 0:1].to_broadcast([P, 64]), op=MULT)
 
         def mask_d():

@@ -24,6 +24,7 @@ CHUNK = 512
 HALF = 256
 TWO_ONES = 0x3F803F80
 PIECES = (("a", 1024, 256), ("b", 1280, 256), (3, 1536, 512), (4, 2048, 512), (5, 2560, 512), (6, 3072, 512), (7, 3584, 512), (0, 0, 512), (1, 512, 512))
+EARLY = (3, 4, 5)
 NCOL = 10
 RUN = 14
 
@@ -56,7 +57,7 @@ def tile_shiftconv_kernel(tc, x, w_pw, out):
         nc.vector.memset(direct_w[:], 0.0)
         nc.vector.quantize_mx(out=warm_codes[:].bitcast(FP8X4), scales=warm_scales[:], in_=warm_in[:])
         idle = ps_mx.tile([P, 4, P], F32, tag="acc", name="idle")
-        for k in range(20):
+        for k in range(18):
             nc.tensor.matmul_mx(
                 out=idle[:, k % 4, :],
                 lhsT=warm_codes[:].bitcast(FP8X4),
@@ -70,12 +71,12 @@ def tile_shiftconv_kernel(tc, x, w_pw, out):
         x_flat = x.rearrange("b c h w -> (b c h w)")
         out_v = out.rearrange("b (o t) h w -> o (b t) (h w)", t=4)
 
-        spans = {"a": (QUARTER, CHUNK), "b": (QUARTER + CHUNK, CHUNK), "c": (2 * QUARTER, 2 * QUARTER), "d": (0, QUARTER)}
+        spans = {"a": (QUARTER, HALF), "b": (QUARTER + HALF, 3 * HALF), "c": (2 * QUARTER, 2 * QUARTER), "d": (0, QUARTER)}
         xs = {}
         for name, (first, n) in spans.items():
             xs[name] = keep.tile([P, 2, n], BF16, name="x_%s" % name)
-        x4a = keep.tile([P, CHUNK], BF16, name="x4a")
-        x4b = keep.tile([P, CHUNK], BF16, name="x4b")
+        x4a = keep.tile([P, HALF], BF16, name="x4a")
+        x4b = keep.tile([P, 3 * HALF], BF16, name="x4b")
         w_sb = keep.tile([P, 4, 512], BF16, name="w_sb")
         fix_in = keep.tile([P, 16], BF16, name="fix_in")
         fix = keep.tile([P, P], BF16, name="fix")
@@ -105,11 +106,11 @@ def tile_shiftconv_kernel(tc, x, w_pw, out):
         x4_rows = x_flat[first_channel(4) * CH : first_channel(4) * CH + P * QUARTER].rearrange("(r l) -> r l", l=QUARTER)
         for e in range(4):
             load_pair(e, "a")
-        nc.sync.dma_start(out=x4a[:], in_=x4_rows[:, 0:CHUNK])
+        nc.sync.dma_start(out=x4a[:], in_=x4_rows[:, 0:HALF])
         nc.scalar.dma_start(out=w_sb[:], in_=w_pw.rearrange("(o t) c -> o t c", t=4))
         for e in range(4):
             load_pair(e, "b")
-        nc.sync.dma_start(out=x4b[:], in_=x4_rows[:, CHUNK:QUARTER])
+        nc.sync.dma_start(out=x4b[:], in_=x4_rows[:, HALF:QUARTER])
         for e in range(4):
             load_pair(e, "c")
 
@@ -193,7 +194,7 @@ def tile_shiftconv_kernel(tc, x, w_pw, out):
 
         def x4_window(first, n):
             col = first % QUARTER
-            return x4a[:, col : col + n] if col < CHUNK else x4b[:, col - CHUNK : col - CHUNK + n]
+            return x4a[:, col : col + n] if col < HALF else x4b[:, col - HALF : col - HALF + n]
 
         def direct(piece):
             first, n, t, lo = pieces[piece]
@@ -257,22 +258,31 @@ def tile_shiftconv_kernel(tc, x, w_pw, out):
                 )
 
         def round_piece(piece):
-            n = NCOL * pieces[piece][1] // P
-            twin = keep.tile([P, n, 2], BF16, name="twin%s" % piece)
-            m = n // NCOL
-            nc.vector.tensor_tensor(
-                out=twin[:].rearrange("p (t g) j -> p t g j", g=NCOL),
-                in0=rows[piece].rearrange("p (t g) -> p t g", g=NCOL).unsqueeze(3).to_broadcast([P, m, NCOL, 2]),
-                in1=kept[:].unsqueeze(1).unsqueeze(3).to_broadcast([P, m, NCOL, 2]),
-                op=MULT,
-            )
-            twins[piece] = twin
+            tiles = pieces[piece][1] // P
+            twins[piece] = keep.tile([P, tiles * NCOL, 2], BF16, name="twin%s" % piece)
+            step = tiles // 2 if piece in EARLY else tiles
+            for lo in range(0, tiles, step):
+                part = slice(NCOL * lo, NCOL * (lo + step))
+                nc.vector.tensor_tensor(
+                    out=twins[piece][:, part, :].rearrange("p (t g) j -> p t g j", g=NCOL),
+                    in0=rows[piece][:, part]
+                    .rearrange("p (t g) -> p t g", g=NCOL)
+                    .unsqueeze(3)
+                    .to_broadcast([P, step, NCOL, 2]),
+                    in1=kept[:].unsqueeze(1).unsqueeze(3).to_broadcast([P, step, NCOL, 2]),
+                    op=MULT,
+                )
 
         def spread_piece(piece):
-            n = NCOL * pieces[piece][1] // P
-            wide = keep.tile([P, n, RUN], F32, name="wide%s" % piece)
+            tiles = pieces[piece][1] // P
+            wide = keep.tile([P, tiles * NCOL, RUN], F32, name="wide%s" % piece)
             src = twins[piece][:].rearrange("p g j -> p (g j)").bitcast(F32)
-            nc.vector.tensor_copy(out=wide[:], in_=src.unsqueeze(2).to_broadcast([P, n, RUN]))
+            step = tiles // 2 if piece in EARLY else tiles
+            for lo in range(0, tiles, step):
+                part = slice(NCOL * lo, NCOL * (lo + step))
+                nc.vector.tensor_copy(
+                    out=wide[:, part, :], in_=src[:, part].unsqueeze(2).to_broadcast([P, NCOL * step, RUN])
+                )
             spreads[piece] = wide[:].rearrange("p g s -> p (g s)")
 
         def flip_piece(piece):
@@ -344,9 +354,10 @@ def tile_shiftconv_kernel(tc, x, w_pw, out):
             nc.gpsimd.tensor_tensor(out=top, in0=top, in1=sel[:, 0, 3:4].to_broadcast([P, 64]), op=MULT)
             nc.gpsimd.tensor_copy(out=fix[:, 65:66], in_=fix_in[:, 0:1])
 
+        mask_edges(nc.vector, "a")
+        mask_edges(nc.gpsimd, "b")
         mask_c()
         mask_d()
-        mask_edges(nc.vector, "a")
         make_kept()
         direct("a")
         w_flip(0)
@@ -385,7 +396,7 @@ def tile_shiftconv_kernel(tc, x, w_pw, out):
             for j in (range(i + 3, i + 5) if i == 1 else range(i + 3 + min(i, 1), i + 4 + min(i, 1))):
                 if j < len(seq):
                     sum_piece(seq[j])
-            evict(p, 0, True)
+            evict(p, 0, p != "b")
             evict(p, 1, False)
             if nxt is not None:
                 quantise(nxt)

@@ -57,7 +57,7 @@ def tile_shiftconv_kernel(tc, x, w_pw, out):
         nc.vector.memset(direct_w[:], 0.0)
         nc.vector.quantize_mx(out=warm_codes[:].bitcast(FP8X4), scales=warm_scales[:], in_=warm_in[:])
         idle = ps_mx.tile([P, 4, P], F32, tag="acc", name="idle")
-        for k in range(18):
+        for k in range(15):
             nc.tensor.matmul_mx(
                 out=idle[:, k % 4, :],
                 lhsT=warm_codes[:].bitcast(FP8X4),
@@ -168,9 +168,12 @@ def tile_shiftconv_kernel(tc, x, w_pw, out):
             )
 
         def mask_edges(engine, name):
-            rows = spans[name][1] // 64
-            v = xs[name][:].rearrange("p k (h w) -> p k h w", w=64)[:, :, :, 0:64:63]
-            engine.tensor_tensor(out=v, in0=v, in1=edge_v.unsqueeze(2).to_broadcast([P, 2, rows, 2]), op=MULT)
+            rows = HALF // 64
+            for k in range(2):
+                v = xs[name][:, k, 0:HALF].rearrange("p (h w) -> p h w", w=64)[:, :, 0:64:63]
+                engine.tensor_tensor(
+                    out=v, in0=v, in1=edge_v[:, k].unsqueeze(1).to_broadcast([P, rows, 2]), op=MULT
+                )
 
         pieces = {}
         for name, first, n in PIECES:
@@ -367,44 +370,60 @@ def tile_shiftconv_kernel(tc, x, w_pw, out):
         w_copy(1, False)
         w_flip(2)
         w_flip(3)
+        sum_piece(3)
         direct("b")
         quantise("a")
         w_quantise(0)
         w_copy(2, False)
         w_quantise(1)
-        w_copy(3, True)
-        sum_piece(3)
+        w_copy(3, False)
+        round_piece(3)
+        spread_piece(3)
+        multiply_bank("a", 0)
+        w_quantise(2)
+        w_quantise(3)
+        expand("b")
+        flip_piece(3)
+        multiply_bank("a", 1)
+        evict("a", 0, True)
+        expand(3)
+        sum_piece(4)
+        quantise("b")
+        evict("a", 1, False)
+        multiply_bank("b", 0)
+        round_piece(4)
+        spread_piece(4)
+        multiply_bank("b", 1)
+        evict("b", 0, False)
+        flip_piece(4)
+        quantise(3)
+        evict("b", 1, True)
+        sum_piece(5)
+        sum_piece(6)
+        round_piece(5)
+        spread_piece(5)
         seq = ("a", "b", 3, 4, 5, 6, 7, 0, 1)
-        for i, p in enumerate(seq):
-            banks = 4 * pieces[p][1] // CHUNK
+        for i in range(2, len(seq)):
+            p = seq[i]
             nxt = seq[i + 1] if i + 1 < len(seq) else None
             sec = seq[i + 2] if i + 2 < len(seq) else None
             thd = seq[i + 3] if i + 3 < len(seq) else None
             multiply_bank(p, 0)
             if nxt is not None:
                 expand(nxt)
-            if i == 0:
-                w_quantise(2)
-                w_quantise(3)
-                round_piece(3)
-            for bank in range(1, banks):
+            for bank in range(1, 4):
                 multiply_bank(p, bank)
-            if i == 0:
-                spread_piece(3)
             if sec is not None:
                 flip_piece(sec)
-            for j in (range(i + 3, i + 5) if i == 1 else range(i + 3 + min(i, 1), i + 4 + min(i, 1))):
-                if j < len(seq):
-                    sum_piece(seq[j])
-            evict(p, 0, p != "b")
+            if i + 4 < len(seq):
+                sum_piece(seq[i + 4])
+            evict(p, 0, True)
             evict(p, 1, False)
             if nxt is not None:
                 quantise(nxt)
-            if banks == 4:
-                evict(p, 2, False)
+            evict(p, 2, False)
             if thd is not None:
                 round_piece(thd)
-            if banks == 4:
-                evict(p, 3, True)
+            evict(p, 3, True)
             if thd is not None:
                 spread_piece(thd)

@@ -49,24 +49,13 @@ def tile_shiftconv_kernel(tc, x, w_pw, out):
         ctx.enter_context(tc.manual_schedule())
         ctx.enter_context(nc.allow_low_precision(reason="sums of one nonzero term, exact in bfloat16"))
 
-        warm_in = keep.tile([P, 512], BF16, name="warm_in", align_bytes=64)
-        warm_codes = keep.tile([P, P], U32, name="warm_codes", align_bytes=64)
-        warm_scales = keep.tile([P, P], U8, name="warm_scales", align_bytes=64)
+        warm_in = keep.tile([P, P], BF16, name="warm_in")
         nc.vector.memset(warm_in[:].bitcast(I32), TWO_ONES)
         direct_w = keep.tile([P, 512], BF16, name="direct_w")
         nc.vector.memset(direct_w[:], 0.0)
-        nc.vector.quantize_mx(out=warm_codes[:].bitcast(FP8X4), scales=warm_scales[:], in_=warm_in[:])
         idle = ps_mx.tile([P, 4, P], F32, tag="acc", name="idle")
-        for k in range(15):
-            nc.tensor.matmul_mx(
-                out=idle[:, k % 4, :],
-                lhsT=warm_codes[:].bitcast(FP8X4),
-                lhsT_scale=warm_scales[:],
-                rhs=warm_codes[:].bitcast(FP8X4),
-                rhs_scale=warm_scales[:],
-                start=True,
-                stop=True,
-            )
+        for k in range(19):
+            nc.tensor.matmul(idle[:, k % 4, :], lhsT=warm_in[:], rhs=warm_in[:], start=True, stop=True)
 
         x_flat = x.rearrange("b c h w -> (b c h w)")
         out_v = out.rearrange("b (o t) h w -> o (b t) (h w)", t=4)

from contextlib import ExitStack

import concourse.mybir as mybir
from concourse.masks import make_identity

FLOPS = 2 * 512 * 512 * 4096

BF16 = mybir.dt.bfloat16
F32 = mybir.dt.float32
I32 = mybir.dt.int32
U8 = mybir.dt.uint8
U32 = mybir.dt.uint32
FP8X4 = mybir.dt.float8_e4m3fn_x4
ADD = mybir.AluOpType.add
MULT = mybir.AluOpType.mult
EQ = mybir.AluOpType.is_equal
AX = mybir.AxisListType.X
AXY = mybir.AxisListType.XY

P = 128
CH = 4096
QUARTER = 1024
CHUNK = 512
HALF = 256
TWO_ONES = 0x3F803F80
PIECES = (("a", 1024, 256), ("b", 1280, 256), (3, 1536, 512), (4, 2048, 512), (5, 2560, 512), (6, 3072, 512), (7, 3584, 512), (0, 0, 512), (1, 512, 512))
EARLY = (3, 4, 5)
NCOL = 10
RUN = 14


def shift_of(g):
    return 64 * (g // 3 - 1) + (g % 3 - 1)


def first_channel(g):
    if g == 8:
        return 28 * g - 4
    return 28 * g


def tile_shiftconv_kernel(tc, x, w_pw, out):
    nc = tc.nc
    with ExitStack() as ctx:
        keep = ctx.enter_context(tc.tile_pool(name="keep", bufs=1))
        ps_sum = ctx.enter_context(tc.psum_pool(name="ps_sum", bufs=2))
        ps_aux = ctx.enter_context(tc.psum_pool(name="ps_aux", bufs=2))
        ps_mx = ctx.enter_context(tc.psum_pool(name="ps_mx", bufs=4))
        ctx.enter_context(tc.manual_schedule())
        ctx.enter_context(nc.allow_low_precision(reason="sums of one nonzero term, exact in bfloat16"))

        warm_in = keep.tile([P, P], BF16, name="warm_in")
        nc.vector.memset(warm_in[:].bitcast(I32), TWO_ONES)
        direct_w = keep.tile([P, 512], BF16, name="direct_w")
        nc.vector.memset(direct_w[:], 0.0)
        idle = ps_mx.tile([P, 4, P], F32, tag="acc", name="idle")
        for k in range(19):
            nc.tensor.matmul(idle[:, k % 4, :], lhsT=warm_in[:], rhs=warm_in[:], start=True, stop=True)

        x_flat = x.rearrange("b c h w -> (b c h w)")
        out_v = out.rearrange("b (o t) h w -> o (b t) (h w)", t=4)

        spans = {"a": (QUARTER, HALF), "b": (QUARTER + HALF, 3 * HALF), "c": (2 * QUARTER, 2 * QUARTER), "d": (0, QUARTER)}
        xs = {}
        for name, (first, n) in spans.items():
            xs[name] = keep.tile([P, 2, n], BF16, name="x_%s" % name)
        x4a = keep.tile([P, HALF], BF16, name="x4a")
        x4b = keep.tile([P, 3 * HALF], BF16, name="x4b")
        w_sb = keep.tile([P, 4, 512], BF16, name="w_sb")
        fix_in = keep.tile([P, 16], BF16, name="fix_in")
        fix = keep.tile([P, P], BF16, name="fix")

        def load_pair(e, name):
            first, n = spans[name]
            b = first_channel(e) * CH + shift_of(e) + first
            apart = (first_channel(e + 5) - first_channel(e)) * CH + shift_of(e + 5) - shift_of(e)
            m = 2 if apart % 2 == 0 else 3
            z = apart // m
            assert z * m == apart
            back = max(0, b + (m + 1) * z - 256 * CH)
            both = x_flat[b - back : b - back + (m + 1) * z].rearrange("(k z) -> k z", z=z)
            (nc.scalar if name == "a" and e % 2 == 1 else nc.sync).dma_start(
                out=xs[name][e:P:4, :, :],
                in_=both[0 : m + 1 : m, back : back + 32 * CH].rearrange("k (r c) -> r k c", c=CH)[:, :, 0:n],
            )

        def load_one(g, name, skip):
            first, n = spans[name]
            b = first_channel(g) * CH + shift_of(g) + first + skip
            nc.sync.dma_start(
                out=xs[name][g % 5 : P : 4, g // 5, skip:n],
                in_=x_flat[b : b + 32 * CH].rearrange("(r c) -> r c", c=CH)[:, 0 : n - skip],
            )

        x4_rows = x_flat[first_channel(4) * CH : first_channel(4) * CH + P * QUARTER].rearrange("(r l) -> r l", l=QUARTER)
        for e in range(4):
            load_pair(e, "a")
        nc.sync.dma_start(out=x4a[:], in_=x4_rows[:, 0:HALF])
        nc.scalar.dma_start(out=w_sb[:], in_=w_pw.rearrange("(o t) c -> o t c", t=4))
        for e in range(4):
            load_pair(e, "b")
        nc.sync.dma_start(out=x4b[:], in_=x4_rows[:, HALF:QUARTER])
        for e in range(4):
            load_pair(e, "c")

        ident = keep.tile([P, P], F32, name="ident")
        make_identity(nc, ident[:])
        nc.gpsimd.memset(xs["d"][:, 0, 0:80], 0.0)
        nc.gpsimd.memset(fix_in[:], 0.0)
        nc.gpsimd.memset(fix[:], 0.0)

        for e in range(1, 4):
            load_pair(e, "d")
        load_one(5, "d", 0)
        load_one(0, "d", 66)
        nc.sync.dma_start(
            out=fix_in[0:P:4, 0:2], in_=x_flat[0 : 32 * CH].rearrange("(r c) -> r c", c=CH)[:, 0:2]
        )

        sel = keep.tile([P, 2, 4], BF16, name="sel")
        edge = keep.tile([P, 4], BF16, name="edge")
        nc.vector.tensor_reduce(
            out=sel[:],
            in_=ident[:, 0:112].rearrange("p (c e) -> p e c", e=4).unsqueeze(1).to_broadcast([P, 2, 4, 28]),
            axis=AX,
            op=ADD,
        )
        nc.vector.tensor_reduce(
            out=edge[:, 0:4:3],
            in_=ident[:].rearrange("p (c e) -> p c e", e=4)[:, :, 1:3].unsqueeze(1).to_broadcast([P, 2, 32, 2]),
            axis=AXY,
            op=ADD,
        )
        nc.vector.tensor_reduce(out=sel[:, 1, 3:4], in_=ident[:, 19:128:4], axis=AX, op=ADD)
        nc.vector.tensor_scalar(out=edge[:, 1:3], in0=sel[:, 0, 1:3], scalar1=0.0, scalar2=None, op0=EQ)
        runs = direct_w[:, 0:396].rearrange("p (k z) -> p k z", z=198)[:, :, 0:56].rearrange(
            "p k (e s) -> p k e s", s=RUN
        )
        nc.vector.tensor_copy(out=runs, in_=sel[:].unsqueeze(3).to_broadcast([P, 2, 4, RUN]))
        nc.vector.tensor_copy(out=direct_w[:, 256 + 56 : 256 + 70], in_=sel[:, 0, 1:2].to_broadcast([P, RUN]))
        nc.vector.tensor_copy(out=direct_w[:, 256 + 126 : 256 + 128], in_=sel[:, 0, 1:2].to_broadcast([P, 2]))
        edge_v = edge[:].rearrange("p (w k) -> p k w", k=2)

        ends = keep.tile([P, 2], F32, name="ends")
        kept = keep.tile([P, NCOL], F32, name="kept")

        nc.gpsimd.memset(kept[:], 1.0)

        def make_kept():
            nc.vector.tensor_reduce(
                out=ends[:], in_=ident[:].rearrange("p (h w) -> p w h", w=64)[:, 0:64:63, :], axis=AX, op=ADD
            )
            nc.vector.tensor_scalar(out=ends[:], in0=ends[:], scalar1=0.0, scalar2=None, op0=EQ)
            nc.vector.tensor_copy(
                out=kept[:, 0:9].rearrange("p (i j) -> p i j", j=3)[:, :, 0:3:2],
                in_=ends[:].unsqueeze(1).to_broadcast([P, 3, 2]),
            )

        def mask_edges(engine, name):
            rows = HALF // 64
            for k in range(2):
                v = xs[name][:, k, 0:HALF].rearrange("p (h w) -> p h w", w=64)[:, :, 0:64:63]
                engine.tensor_tensor(
                    out=v, in0=v, in1=edge_v[:, k].unsqueeze(1).to_broadcast([P, rows, 2]), op=MULT
                )

        pieces = {}
        for name, first, n in PIECES:
            for t, (lo, m) in spans.items():
                if lo <= first < lo + m:
                    pieces[name] = (first, n, t, first - lo)
        used = [0]
        rows = {}
        gw = keep.tile([P, 4, P, 2], F32, name="gw", align_bytes=64)
        w_codes = keep.tile([P, 512], U32, name="w_codes", align_bytes=64)
        w_scales = keep.tile([P, 512], U8, name="w_scales", align_bytes=64)
        wts = {}
        twins = {}
        spreads = {}
        pairs = {}
        groupeds = {}
        codes = {}
        scales = {}
        accs = {}
        results = {}

        def x4_window(first, n):
            col = first % QUARTER
            return x4a[:, col : col + n] if col < HALF else x4b[:, col - HALF : col - HALF + n]

        def direct(piece):
            first, n, t, lo = pieces[piece]
            dp = ps_aux.tile([P, 2 * n], BF16, tag="aux", name="dp%s" % piece)
            for h in range(n // HALF):
                for i in range(3):
                    if i < 2:
                        window = xs[t][:, i, lo + HALF * h : lo + HALF * (h + 1)]
                    else:
                        window = x4_window(first + HALF * h, HALF)
                    nc.tensor.matmul(
                        dp[:, CHUNK * h : CHUNK * (h + 1)].rearrange("p (n j) -> p n j", j=2),
                        lhsT=direct_w[:, P * i : P * (i + 1)],
                        rhs=window.unsqueeze(2).to_broadcast([P, HALF, 2]),
                        start=i == 0,
                        stop=i == 2,
                    )
            pairs[piece] = dp[:].bitcast(F32)

        def w_flip(t):
            wt = ps_mx.tile([P, 2, P], F32, tag="acc", name="wt%d" % t)
            words = w_sb[:, t, :].bitcast(F32).rearrange("o (p u) -> o u p", u=2)
            for u in range(2):
                nc.tensor.transpose(wt[:, u, :], words[:, u, :], ident[:])
            wts[t] = wt

        def w_copy(t, on_vector):
            src = wts[t][:].rearrange("p u o -> p o u")
            if on_vector:
                nc.vector.tensor_copy(out=gw[:, t, :, :], in_=src)
            else:
                nc.scalar.copy(out=gw[:, t, :, :], in_=src)

        def w_quantise(t):
            cols = slice(P * t, P * (t + 1))
            nc.vector.quantize_mx(
                out=w_codes[:, cols].bitcast(FP8X4),
                scales=w_scales[:, cols],
                in_=gw[:, t, :, :].rearrange("p o u -> p (o u)").bitcast(BF16),
            )

        def sum_piece(piece):
            first, n, t, lo = pieces[piece]
            q = first // QUARTER
            sums = ps_sum.tile([P, n // P, NCOL], F32, tag="sums", name="sums%s" % piece)
            rows[piece] = sums[:].rearrange("p t g -> p (t g)")
            for k in range(n // P):
                row = sums[:, k, :]
                top = first + k == 0
                at = lo + P * k
                nc.tensor.matmul(row[:, 0:4], lhsT=xs[t][:, 0, at : at + P], rhs=sel[:, 0, :], start=True, stop=not top)
                if top:
                    nc.tensor.matmul(row[:, 0:4], lhsT=fix[:], rhs=sel[:, 0, :], start=False, stop=True)
                nc.tensor.matmul(row[:, 5:9], lhsT=xs[t][:, 1, at : at + P], rhs=sel[:, 1, :], start=True, stop=True)
                nc.tensor.matmul(
                    row[:, 4:10:5],
                    lhsT=x4_window(first + P * k, P),
                    rhs=sel[:, 0, q : q + 1].to_broadcast([P, 2]),
                    start=True,
                    stop=True,
                )

        def round_piece(piece):
            tiles = pieces[piece][1] // P
            twins[piece] = keep.tile([P, tiles * NCOL, 2], BF16, name="twin%s" % piece)
            step = tiles // 2 if piece in EARLY else tiles
            for lo in range(0, tiles, step):
                part = slice(NCOL * lo, NCOL * (lo + step))
                nc.vector.tensor_tensor(
                    out=twins[piece][:, part, :].rearrange("p (t g) j -> p t g j", g=NCOL),
                    in0=rows[piece][:, part]
                    .rearrange("p (t g) -> p t g", g=NCOL)
                    .unsqueeze(3)
                    .to_broadcast([P, step, NCOL, 2]),
                    in1=kept[:].unsqueeze(1).unsqueeze(3).to_broadcast([P, step, NCOL, 2]),
                    op=MULT,
                )

        def spread_piece(piece):
            tiles = pieces[piece][1] // P
            wide = keep.tile([P, tiles * NCOL, RUN], F32, name="wide%s" % piece)
            src = twins[piece][:].rearrange("p g j -> p (g j)").bitcast(F32)
            step = tiles // 2 if piece in EARLY else tiles
            for lo in range(0, tiles, step):
                part = slice(NCOL * lo, NCOL * (lo + step))
                nc.vector.tensor_copy(
                    out=wide[:, part, :], in_=src[:, part].unsqueeze(2).to_broadcast([P, NCOL * step, RUN])
                )
            spreads[piece] = wide[:].rearrange("p g s -> p (g s)")

        def flip_piece(piece):
            n = pieces[piece][1] // P
            pt = ps_aux.tile([P, n, P], F32, tag="aux", name="pt%s" % piece)
            for k in range(n):
                first = NCOL * RUN * k
                nc.tensor.transpose(pt[:, k, :], spreads[piece][:, first : first + P], ident[:])
            pairs[piece] = pt[:].rearrange("p t n -> p (t n)")

        def expand(piece):
            n = pieces[piece][1]
            grouped = keep.tile([P, 4 * n], BF16, name="grouped%s" % piece, align_bytes=64)
            nc.scalar.copy(
                out=grouped[:].bitcast(F32).rearrange("p (n j) -> p n j", j=2),
                in_=pairs[piece].unsqueeze(2).to_broadcast([P, n, 2]),
            )
            groupeds[piece] = grouped

        def quantise(piece):
            n = pieces[piece][1]
            cd = keep.tile([P, n], U32, name="codes%s" % piece, align_bytes=64)
            sc = keep.tile([P, n], U8, name="scales%s" % piece, align_bytes=64)
            nc.vector.quantize_mx(out=cd[:].bitcast(FP8X4), scales=sc[:], in_=groupeds[piece][:])
            codes[piece] = cd
            scales[piece] = sc

        def multiply_bank(piece, bank):
            n = pieces[piece][1]
            per_bank = CHUNK // n
            acc = ps_mx.tile([P, per_bank, n], F32, tag="acc", name="acc%s_%d" % (piece, bank))
            accs[(piece, bank)] = acc
            for k in range(per_bank):
                ot = per_bank * bank + k
                nc.tensor.matmul_mx(
                    out=acc[:, k, :],
                    lhsT=w_codes[:, P * ot : P * (ot + 1)].bitcast(FP8X4),
                    lhsT_scale=w_scales[:, P * ot : P * (ot + 1)],
                    rhs=codes[piece][:].bitcast(FP8X4),
                    rhs_scale=scales[piece][:],
                    start=True,
                    stop=True,
                )

        def evict(piece, bank, on_vector):
            first, n, _, _ = pieces[piece]
            per_bank = CHUNK // n
            whole = 2 if n == CHUNK else 1
            if bank % whole == 0:
                results[piece] = keep.tile([P, whole * per_bank, n], F32, name="res%s_%d" % (piece, bank))
            at = per_bank * (bank % whole)
            dst = results[piece][:, at : at + per_bank, :]
            if on_vector:
                nc.vector.tensor_copy(out=dst, in_=accs[(piece, bank)][:])
            else:
                nc.scalar.copy(out=dst, in_=accs[(piece, bank)][:])
            if bank % whole == whole - 1:
                lo = per_bank * (bank + 1 - whole)
                nc.sync.dma_start(
                    out=out_v[:, lo : lo + whole * per_bank, first : first + n], in_=results[piece][:]
                )

        def mask_c():
            bottom = xs["c"][:, 1, 2 * QUARTER - 64 : 2 * QUARTER]
            nc.gpsimd.tensor_tensor(out=bottom, in0=bottom, in1=sel[:, 1, 0:1].to_broadcast([P, 64]), op=MULT)

        def mask_d():
            top = xs["d"][:, 0, 0:64]
            nc.gpsimd.tensor_tensor(out=top, in0=top, in1=sel[:, 0, 3:4].to_broadcast([P, 64]), op=MULT)
            nc.gpsimd.tensor_copy(out=fix[:, 65:66], in_=fix_in[:, 0:1])

        mask_edges(nc.vector, "a")
        mask_edges(nc.gpsimd, "b")
        mask_c()
        mask_d()
        make_kept()
        direct("a")
        w_flip(0)
        w_flip(1)
        expand("a")
        w_copy(0, True)
        w_copy(1, False)
        w_flip(2)
        w_flip(3)
        sum_piece(3)
        direct("b")
        quantise("a")
        w_quantise(0)
        w_copy(2, False)
        w_quantise(1)
        w_copy(3, False)
        round_piece(3)
        spread_piece(3)
        multiply_bank("a", 0)
        w_quantise(2)
        w_quantise(3)
        expand("b")
        flip_piece(3)
        multiply_bank("a", 1)
        evict("a", 0, True)
        expand(3)
        sum_piece(4)
        quantise("b")
        evict("a", 1, False)
        multiply_bank("b", 0)
        round_piece(4)
        spread_piece(4)
        multiply_bank("b", 1)
        evict("b", 0, False)
        flip_piece(4)
        quantise(3)
        evict("b", 1, True)
        sum_piece(5)
        sum_piece(6)
        round_piece(5)
        spread_piece(5)
        seq = ("a", "b", 3, 4, 5, 6, 7, 0, 1)
        for i in range(2, len(seq)):
            p = seq[i]
            nxt = seq[i + 1] if i + 1 < len(seq) else None
            sec = seq[i + 2] if i + 2 < len(seq) else None
            thd = seq[i + 3] if i + 3 < len(seq) else None
            multiply_bank(p, 0)
            if nxt is not None:
                expand(nxt)
            for bank in range(1, 4):
                multiply_bank(p, bank)
            if sec is not None:
                flip_piece(sec)
            if i + 4 < len(seq):
                sum_piece(seq[i + 4])
            evict(p, 0, True)
            evict(p, 1, False)
            if nxt is not None:
                quantise(nxt)
            evict(p, 2, False)
            if thd is not None:
                round_piece(thd)
            evict(p, 3, True)
            if thd is not None:
                spread_piece(thd)
